import numpy as np
import ml_dtypes


def mxq(x, axis, fmt="e4m3"):
    dtype, down = {"e4m3": (ml_dtypes.float8_e4m3fn, 7), "e5m2": (ml_dtypes.float8_e5m2, 14)}[fmt]
    v = np.moveaxis(np.asarray(x, np.float32).astype(ml_dtypes.bfloat16).astype(np.float64), axis, -1)
    blocks = v.reshape(v.shape[:-1] + (-1, 32))
    amax = np.abs(blocks).max(-1, keepdims=True)
    byte = np.maximum(np.where(amax > 0, np.frexp(amax)[1] - 1 + 127, 0) - down, 1)
    scale = np.exp2(byte - 127.0)
    codes = (blocks / scale).astype(np.float32).astype(dtype).astype(np.float64)
    return np.moveaxis((codes * scale).reshape(v.shape), -1, axis)


WIDE = False


def mx_kscale(k):
    if not WIDE:
        return np.ones(k)
    levels = np.array([10, -10, 5, -5, 0])
    a = np.random.permutation(np.resize(levels, k // 512 * 4)).reshape(k // 512, 4)
    idx = np.arange(k)
    return np.exp2(a[idx // 512, idx % 128 // 32])


BF16 = ml_dtypes.bfloat16


def bf(x):
    return np.asarray(x, np.float32).astype(BF16)


def f64(x):
    return np.asarray(x).astype(np.float64)


E2M1 = np.array([0.0, 0.5, 1.0, 1.5, 2.0, 3.0, 4.0, 6.0, -0.0, -0.5, -1.0, -1.5, -2.0, -3.0, -4.0, -6.0])


def pack_weight(w, fmt):
    k, n = w.shape
    w = f64(bf(w)).reshape(k // 32, 32, n)
    amax = np.abs(w).max(1)
    if fmt == "e4m3":
        byte = np.frexp(amax)[1] - 1 + 127 - 7
    else:
        mant, ex = np.frexp(amax / 6.0)
        byte = np.where(mant > 0.5, ex, ex - 1) + 127
    byte = np.clip(np.where(amax > 0, byte, 1), 1, 254)
    scaled = (w * np.exp2(127.0 - byte)[:, None, :]).reshape(k, n).astype(np.float32)
    by_word = np.ascontiguousarray(scaled.reshape(k // 512, 128, 4, n).transpose(0, 1, 3, 2))
    if fmt == "e4m3":
        words = by_word.astype(ml_dtypes.float8_e4m3fn).view(np.uint8)
    else:
        c = by_word.astype(ml_dtypes.float4_e2m1fn).view(np.uint8) & 0xF
        words = c[..., 0::2] | (c[..., 1::2] << 4)
    return np.ascontiguousarray(words), np.ascontiguousarray(byte.astype(np.uint8).reshape(k // 512, 16, n))


def unpack_weight(words, scales, fmt):
    g, p, n, _ = words.shape
    if fmt == "e4m3":
        vals = np.ascontiguousarray(words).view(ml_dtypes.float8_e4m3fn).astype(np.float64)
    else:
        nib = np.empty((g, p, n, 4), np.uint8)
        nib[..., 0::2] = words & 0xF
        nib[..., 1::2] = words >> 4
        vals = E2M1[nib]
    vals = vals * np.repeat(np.exp2(scales.astype(np.float64) - 127.0), 8, axis=1)[..., None]
    return vals.transpose(0, 1, 3, 2).reshape(g * 512, n)


B, IN_DIM, MEM = 2048, 3840, 256
DIN = MEM + IN_DIM
MIN_TS, MAX_TS, EPS = 0.1, 10.0, 1e-6


def sigmoid(v):
    return 1.0 / (1.0 + np.exp(-v))


def setup_inputs():
    s = mx_kscale(DIN)[MEM:]
    r = np.concatenate([np.ones(MEM), s])
    x = bf(np.random.standard_normal((B, IN_DIM)) * s)
    h = bf(np.random.standard_normal((B, MEM)))
    h_candidate = bf(np.tanh(0.7 * np.random.standard_normal((B, MEM))))
    Wd_words, Wd_scales = pack_weight(np.random.standard_normal((DIN, MEM)) * 1.3 / np.sqrt(DIN) / r[:, None], "e4m3")
    bd = bf(np.random.standard_normal(MEM) * 0.5)
    Wu_words, Wu_scales = pack_weight(np.random.standard_normal((DIN, MEM)) * 1.3 / np.sqrt(DIN) / r[:, None], "e4m3")
    bu = bf(np.random.standard_normal(MEM) * 0.5)
    return {"x": x,
            "h": h,
            "h_candidate": h_candidate,
            "Wd_words": Wd_words,
            "Wd_scales": Wd_scales,
            "bd": bd,
            "Wu_words": Wu_words,
            "Wu_scales": Wu_scales,
            "bu": bu}


def reference(x, h, h_candidate, Wd_words, Wd_scales, bd, Wu_words, Wu_scales, bu):
    h = f64(h)
    cq = mxq(np.concatenate([h, f64(x)], axis=-1), 1, "e4m3")
    decay = sigmoid((cq @ unpack_weight(Wd_words, Wd_scales, "e4m3")) + f64(bd))
    update = sigmoid((cq @ unpack_weight(Wu_words, Wu_scales, "e4m3")) + f64(bu))
    decay = MIN_TS + (MAX_TS - MIN_TS) * decay + EPS
    new_h = (1.0 - update) * (h / decay) + update * f64(h_candidate)
    h_norm = np.maximum(np.sqrt(np.square(h).sum(-1, keepdims=True)), EPS)
    nh_norm = np.maximum(np.sqrt(np.square(new_h).sum(-1, keepdims=True)), 1e-12)
    return new_h / nh_norm * h_norm

@@ -1,0 +1,247 @@
+import math
+from contextlib import ExitStack
+
+import concourse.mybir as mybir
+from concourse.masks import make_identity
+
+F32 = mybir.dt.float32
+BF16 = mybir.dt.bfloat16
+I32 = mybir.dt.int32
+U32 = mybir.dt.uint32
+U8 = mybir.dt.uint8
+FP8X4 = mybir.dt.float8_e4m3fn_x4
+ALU = mybir.AluOpType
+ACT = mybir.ActivationFunctionType
+
+P = 128
+ROWS, IN_DIM, MEM = 2048, 3840, 256
+DIN = MEM + IN_DIM
+GATES = 2 * MEM
+TILES = ROWS // P
+K_PASS = 4 * P
+GROUPS = DIN // K_PASS
+WORDS = K_PASS // 2
+BANK_GROUPS = 2
+BANKS = GROUPS // BANK_GROUPS
+HALF_GROUPS = GROUPS // 2
+
+FLOPS = 2 * ROWS * DIN * GATES
+
+TS_FLOOR = 0.1 + 1e-6
+TS_SPAN = 10.0 - 0.1
+SHIFT = math.log((TS_FLOOR + TS_SPAN) / TS_FLOOR)
+S_OFFSET = TS_FLOOR / TS_SPAN
+M_GAIN = TS_FLOOR * (TS_FLOOR + TS_SPAN) / TS_SPAN
+H_NORM_FLOOR = 1e-6
+M_NORM_FLOOR = 1e-12 * M_GAIN
+
+
+def tile_liquidmemorycell_pb_kernel(
+    tc, x, h, h_candidate, Wd_words, Wd_scales, bd, Wu_words, Wu_scales, bu, out
+):
+    nc = tc.nc
+    x_rows = x.rearrange("(p t) k -> p t k", t=TILES)
+    h_rows = h.rearrange("(p t) n -> p t n", t=TILES)
+    out_rows = out.rearrange("(p t) n -> p t n", t=TILES)
+
+    with ExitStack() as stack:
+        stack.enter_context(tc.manual_schedule())
+        keep = stack.enter_context(tc.tile_pool(name="keep", bufs=1))
+        stage = stack.enter_context(tc.tile_pool(name="stage", bufs=2))
+        turned = stack.enter_context(tc.psum_pool(name="turned", bufs=6))
+        sums = stack.enter_context(tc.psum_pool(name="sums", bufs=2))
+
+        w_scales = keep.tile([P, GROUPS, GATES], U8, name="w_scales", align_bytes=64)
+        nc.vector.memset(w_scales[:].bitcast(I32), 0)
+        bias_row = keep.tile([P, GATES], BF16, name="bias_row")
+        nc.vector.memset(bias_row[:], 0.0)
+        ones = keep.tile([P, P], BF16, name="ones")
+        nc.vector.memset(ones[:], 1.0)
+        floors = keep.tile([P, 2], F32, name="floors")
+        nc.vector.memset(floors[:, 0:1], H_NORM_FLOOR * H_NORM_FLOOR)
+        nc.vector.memset(floors[:, 1:2], M_NORM_FLOOR * M_NORM_FLOOR)
+        powers = keep.tile([P, 2], F32, name="powers")
+        nc.vector.memset(powers[:, 0:1], 0.5)
+        nc.vector.memset(powers[:, 1:2], -0.5)
+        identity = keep.tile([P, P], F32, name="identity")
+        make_identity(nc, identity[:])
+
+        nc.scalar.dma_start(out=bias_row[0:1, 0:MEM], in_=bd.unsqueeze(0))
+        nc.scalar.dma_start(out=bias_row[0:1, MEM:GATES], in_=bu.unsqueeze(0))
+        table_warmer = keep.tile([P, 1], F32, name="table_warmer")
+        nc.scalar.activation(out=table_warmer[:], in_=powers[:, 0:1], func=ACT.Sigmoid)
+
+        c_tiles = [keep.tile([P, DIN], BF16, name="c%d" % t) for t in range(TILES)]
+
+        def load_c(t):
+            nc.sync.dma_start(out=c_tiles[t][:, 0:MEM], in_=h_rows[:, t, :])
+            nc.sync.dma_start(out=c_tiles[t][:, MEM:DIN], in_=x_rows[:, t, :])
+
+        w_words = keep.tile([P, GROUPS, GATES], U32, name="w_words", align_bytes=64)
+
+        def load_weights():
+            for gate, scales in enumerate((Wd_scales, Wu_scales)):
+                cols = slice(gate * MEM, (gate + 1) * MEM)
+                for quadrant in range(4):
+                    nc.sync.dma_start(
+                        out=w_scales[32 * quadrant : 32 * quadrant + 4, :, cols].bitcast(I32),
+                        in_=scales[:, 4 * quadrant : 4 * quadrant + 4, :]
+                        .rearrange("g r n -> r g n")
+                        .bitcast(I32),
+                    )
+            for gate, words in enumerate((Wd_words, Wu_words)):
+                cols = slice(gate * MEM, (gate + 1) * MEM)
+                nc.sync.dma_start(
+                    out=w_words[:, :, cols].bitcast(I32),
+                    in_=words.rearrange("g p n i -> p g (n i)").bitcast(I32),
+                )
+
+        candidate = keep.tile([P, TILES, MEM], BF16, name="candidate")
+        load_c(0)
+        load_c(1)
+        load_weights()
+        load_c(2)
+        nc.sync.dma_start(
+            out=candidate[:].rearrange("p t n -> p (t n)"),
+            in_=h_candidate.rearrange("(p t) n -> p (t n)", t=TILES),
+        )
+        for t in range(3, TILES):
+            load_c(t)
+
+        bias_sums = sums.tile([P, GATES], F32, name="bias_sums", tag="sums")
+        nc.tensor.matmul(out=bias_sums[:], lhsT=ones[:], rhs=bias_row[:], start=True, stop=True)
+        bias = keep.tile([P, GATES], F32, name="bias")
+        nc.vector.tensor_scalar(
+            out=bias[:, 0:MEM], in0=bias_sums[:, 0:MEM], scalar1=SHIFT, scalar2=None, op0=ALU.add
+        )
+        nc.vector.tensor_copy(out=bias[:, MEM:GATES], in_=bias_sums[:, MEM:GATES])
+
+        banks, grouped, codes, c_scales, gate_sums = {}, {}, {}, {}, {}
+        stats, logits, shifted, update, kept, blend, scale = {}, {}, {}, {}, {}, {}, {}
+
+        def transpose(t):
+            words = c_tiles[t][:].bitcast(F32)
+            for j in range(BANKS):
+                banks[t, j] = turned.tile([P, BANK_GROUPS, 2, P], F32, name="turned%d_%d" % (t, j), tag="turned")
+                for i in range(BANK_GROUPS):
+                    first = (BANK_GROUPS * j + i) * WORDS
+                    for u in range(2):
+                        nc.tensor.transpose(
+                            banks[t, j][:, i, u, :], words[:, first + u : first + WORDS : 2], identity[:]
+                        )
+
+        def copy_out(t, j):
+            if j == 0:
+                grouped[t] = stage.tile([P, DIN], BF16, name="grouped%d" % t, tag="grouped", align_bytes=64)
+            pairs = grouped[t][:].bitcast(F32).rearrange("p (g r u) -> p g r u", g=GROUPS, u=2)
+            nc.scalar.copy(
+                out=pairs[:, BANK_GROUPS * j : BANK_GROUPS * (j + 1), :, :],
+                in_=banks[t, j][:].rearrange("p g u r -> p g r u"),
+            )
+
+        def square_h(t):
+            stats[t] = keep.tile([P, 2], F32, name="stats%d" % t)
+            h_squares = stage.tile([P, MEM], BF16, name="h_squares%d" % t, tag="h_squares")
+            nc.scalar.activation(
+                out=h_squares[:], in_=c_tiles[t][:, 0:MEM], func=ACT.Square, accum_out=stats[t][:, 0:1]
+            )
+
+        def quantise(t, half):
+            if half == 0:
+                codes[t] = stage.tile([P, GROUPS * P], U32, name="codes%d" % t, tag="codes", align_bytes=64)
+                c_scales[t] = stage.tile([P, GROUPS * P], U8, name="c_scales%d" % t, tag="c_scales", align_bytes=64)
+            width = HALF_GROUPS * P
+            cols = slice(half * width, (half + 1) * width)
+            nc.vector.quantize_mx(
+                out=codes[t][:, cols].bitcast(FP8X4),
+                scales=c_scales[t][:, cols],
+                in_=grouped[t][:, 4 * half * width : 4 * (half + 1) * width],
+            )
+
+        def multiply(t):
+            gate_sums[t] = sums.tile([P, GATES], F32, name="gate_sums%d" % t, tag="sums")
+            for g in range(GROUPS):
+                rows = slice(g * P, (g + 1) * P)
+                nc.tensor.matmul_mx(
+                    out=gate_sums[t][:],
+                    lhsT=codes[t][:, rows].bitcast(FP8X4),
+                    lhsT_scale=c_scales[t][:, rows],
+                    rhs=w_words[:, g, :].bitcast(FP8X4),
+                    rhs_scale=w_scales[:, g, :],
+                    start=(g == 0),
+                    stop=(g == GROUPS - 1),
+                )
+
+        def add_bias(t):
+            logits[t] = stage.tile([P, GATES], F32, name="logits%d" % t, tag="logits")
+            nc.vector.tensor_tensor(out=logits[t][:], in0=gate_sums[t][:], in1=bias[:], op=ALU.add)
+
+        def gates(t):
+            shifted[t] = stage.tile([P, MEM], F32, name="shifted%d" % t, tag="shifted")
+            nc.scalar.activation(out=shifted[t][:], in_=logits[t][:, 0:MEM], func=ACT.Sigmoid, scale=-1.0)
+            update[t] = stage.tile([P, MEM], F32, name="update%d" % t, tag="update")
+            nc.scalar.activation(out=update[t][:], in_=logits[t][:, MEM:GATES], func=ACT.Sigmoid)
+
+        def mix(t):
+            kept[t] = stage.tile([P, MEM], F32, name="kept%d" % t, tag="kept")
+            nc.vector.scalar_tensor_tensor(
+                out=kept[t][:], in0=shifted[t][:], scalar=S_OFFSET, in1=c_tiles[t][:, 0:MEM],
+                op0=ALU.add, op1=ALU.mult,
+            )
+            change = stage.tile([P, MEM], F32, name="change%d" % t, tag="change")
+            nc.vector.scalar_tensor_tensor(
+                out=change[:], in0=candidate[:, t, :], scalar=M_GAIN, in1=kept[t][:],
+                op0=ALU.mult, op1=ALU.subtract,
+            )
+            nc.vector.tensor_tensor(out=change[:], in0=change[:], in1=update[t][:], op=ALU.mult)
+            blend[t] = stage.tile([P, MEM], F32, name="blend%d" % t, tag="blend")
+            nc.vector.tensor_tensor(out=blend[t][:], in0=change[:], in1=kept[t][:], op=ALU.add)
+
+        def square_m(t):
+            m_squares = stage.tile([P, MEM], BF16, name="m_squares%d" % t, tag="m_squares")
+            nc.scalar.activation(out=m_squares[:], in_=blend[t][:], func=ACT.Square, accum_out=stats[t][:, 1:2])
+
+        def norms(t):
+            floored = keep.tile([P, 2], F32, name="floored%d" % t)
+            nc.vector.tensor_tensor(out=floored[:], in0=stats[t][:], in1=floors[:], op=ALU.max)
+            scale[t] = keep.tile([P, 2], F32, name="scale%d" % t)
+            nc.gpsimd.tensor_tensor(out=scale[t][:], in0=floored[:], in1=powers[:], op=ALU.pow)
+
+        def finish(t):
+            result = keep.tile([P, MEM], F32, name="result%d" % t)
+            nc.vector.tensor_scalar(
+                out=result[:], in0=blend[t][:], scalar1=scale[t][:, 0:1], scalar2=scale[t][:, 1:2],
+                op0=ALU.mult, op1=ALU.mult,
+            )
+            nc.sync.dma_start(out=out_rows[:, t, :], in_=result[:])
+
+        def live(t):
+            return 0 <= t < TILES
+
+        for ahead in range(TILES + 3):
+            if live(ahead):
+                transpose(ahead)
+            if live(ahead - 2):
+                add_bias(ahead - 2)
+            if live(ahead - 3):
+                finish(ahead - 3)
+            if live(ahead):
+                copy_out(ahead, 0)
+            if live(ahead - 2):
+                gates(ahead - 2)
+            if live(ahead):
+                for j in range(1, BANKS):
+                    copy_out(ahead, j)
+                square_h(ahead)
+            if live(ahead - 2):
+                mix(ahead - 2)
+            if live(ahead):
+                quantise(ahead, 0)
+            if live(ahead - 2):
+                square_m(ahead - 2)
+            if live(ahead):
+                quantise(ahead, 1)
+            if live(ahead - 2):
+                norms(ahead - 2)
+            if live(ahead - 1):
+                multiply(ahead - 1)

@@ -20,10 +20,11 @@ GATES = 2 * MEM
 TILES = ROWS // P
 K_PASS = 4 * P
 GROUPS = DIN // K_PASS
-WORDS = K_PASS // 2
 BANK_GROUPS = 2
 BANKS = GROUPS // BANK_GROUPS
 HALF_GROUPS = GROUPS // 2
+SCALAR_SORTS = 2
+INPUT_BUFS = 8
 
 FLOPS = 2 * ROWS * DIN * GATES
 
@@ -40,14 +41,13 @@ def tile_liquidmemorycell_pb_kernel(
     tc, x, h, h_candidate, Wd_words, Wd_scales, bd, Wu_words, Wu_scales, bu, out
 ):
     nc = tc.nc
-    x_rows = x.rearrange("(p t) k -> p t k", t=TILES)
-    h_rows = h.rearrange("(p t) n -> p t n", t=TILES)
-    out_rows = out.rearrange("(p t) n -> p t n", t=TILES)
 
     with ExitStack() as stack:
         stack.enter_context(tc.manual_schedule())
         keep = stack.enter_context(tc.tile_pool(name="keep", bufs=1))
+        arrivals = stack.enter_context(tc.tile_pool(name="arrivals", bufs=INPUT_BUFS))
         stage = stack.enter_context(tc.tile_pool(name="stage", bufs=2))
+        leaving = stack.enter_context(tc.tile_pool(name="leaving", bufs=3))
         turned = stack.enter_context(tc.psum_pool(name="turned", bufs=6))
         sums = stack.enter_context(tc.psum_pool(name="sums", bufs=2))
 
@@ -71,11 +71,14 @@ def tile_liquidmemorycell_pb_kernel(
         table_warmer = keep.tile([P, 1], F32, name="table_warmer")
         nc.scalar.activation(out=table_warmer[:], in_=powers[:, 0:1], func=ACT.Sigmoid)
 
-        c_tiles = [keep.tile([P, DIN], BF16, name="c%d" % t) for t in range(TILES)]
+        inputs = {}
 
-        def load_c(t):
-            nc.sync.dma_start(out=c_tiles[t][:, 0:MEM], in_=h_rows[:, t, :])
-            nc.sync.dma_start(out=c_tiles[t][:, MEM:DIN], in_=x_rows[:, t, :])
+        def load_inputs(t):
+            rows = slice(t * P, (t + 1) * P)
+            inputs[t] = arrivals.tile([P, DIN + MEM], BF16, name="inputs%d" % t, tag="inputs")
+            nc.sync.dma_start(out=inputs[t][:, 0:MEM], in_=h[rows, :])
+            nc.sync.dma_start(out=inputs[t][:, MEM:DIN], in_=x[rows, :])
+            nc.sync.dma_start(out=inputs[t][:, DIN : DIN + MEM], in_=h_candidate[rows, :])
 
         w_words = keep.tile([P, GROUPS, GATES], U32, name="w_words", align_bytes=64)
 
@@ -96,38 +99,45 @@ def tile_liquidmemorycell_pb_kernel(
                     in_=words.rearrange("g p n i -> p g (n i)").bitcast(I32),
                 )
 
-        candidate = keep.tile([P, TILES, MEM], BF16, name="candidate")
-        load_c(0)
-        load_c(1)
+        load_inputs(0)
+        load_inputs(1)
         load_weights()
-        load_c(2)
-        nc.sync.dma_start(
-            out=candidate[:].rearrange("p t n -> p (t n)"),
-            in_=h_candidate.rearrange("(p t) n -> p (t n)", t=TILES),
-        )
-        for t in range(3, TILES):
-            load_c(t)
+        for t in range(2, INPUT_BUFS):
+            load_inputs(t)
 
-        bias_sums = sums.tile([P, GATES], F32, name="bias_sums", tag="sums")
-        nc.tensor.matmul(out=bias_sums[:], lhsT=ones[:], rhs=bias_row[:], start=True, stop=True)
         bias = keep.tile([P, GATES], F32, name="bias")
-        nc.vector.tensor_scalar(
-            out=bias[:, 0:MEM], in0=bias_sums[:, 0:MEM], scalar1=SHIFT, scalar2=None, op0=ALU.add
-        )
-        nc.vector.tensor_copy(out=bias[:, MEM:GATES], in_=bias_sums[:, MEM:GATES])
 
-        banks, grouped, codes, c_scales, gate_sums = {}, {}, {}, {}, {}
-        stats, logits, shifted, update, kept, blend, scale = {}, {}, {}, {}, {}, {}, {}
+        def spread_biases():
+            bias_sums = sums.tile([P, GATES], F32, name="bias_sums", tag="sums")
+            nc.tensor.matmul(out=bias_sums[:], lhsT=ones[:], rhs=bias_row[:], start=True, stop=True)
+            nc.vector.tensor_scalar(
+                out=bias[:, 0:MEM], in0=bias_sums[:, 0:MEM], scalar1=SHIFT, scalar2=None, op0=ALU.add
+            )
+            nc.vector.tensor_copy(out=bias[:, MEM:GATES], in_=bias_sums[:, MEM:GATES])
+
+        in_order, banks, grouped, codes, c_scales, gate_sums = {}, {}, {}, {}, {}, {}
+        stats, logits, shifted, update, kept, change, blend, scale = {}, {}, {}, {}, {}, {}, {}, {}
+
+        def sort_views(t):
+            as_loaded = inputs[t][:, 0:DIN].bitcast(F32).rearrange("p (g w u) -> p u g w", g=GROUPS, u=2)
+            return as_loaded, in_order[t][:].rearrange("p g u w -> p u g w")
+
+        def sort_on_vector(t):
+            in_order[t] = stage.tile([P, GROUPS, 2, P], F32, name="in_order%d" % t, tag="in_order")
+            as_loaded, target = sort_views(t)
+            nc.vector.tensor_copy(out=target[:, :, SCALAR_SORTS:, :], in_=as_loaded[:, :, SCALAR_SORTS:, :])
+
+        def sort_on_scalar(t):
+            as_loaded, target = sort_views(t)
+            nc.scalar.copy(out=target[:, :, 0:SCALAR_SORTS, :], in_=as_loaded[:, :, 0:SCALAR_SORTS, :])
 
         def transpose(t):
-            words = c_tiles[t][:].bitcast(F32)
             for j in range(BANKS):
                 banks[t, j] = turned.tile([P, BANK_GROUPS, 2, P], F32, name="turned%d_%d" % (t, j), tag="turned")
                 for i in range(BANK_GROUPS):
-                    first = (BANK_GROUPS * j + i) * WORDS
                     for u in range(2):
                         nc.tensor.transpose(
-                            banks[t, j][:, i, u, :], words[:, first + u : first + WORDS : 2], identity[:]
+                            banks[t, j][:, i, u, :], in_order[t][:, BANK_GROUPS * j + i, u, :], identity[:]
                         )
 
         def copy_out(t, j):
@@ -143,7 +153,7 @@ def tile_liquidmemorycell_pb_kernel(
             stats[t] = keep.tile([P, 2], F32, name="stats%d" % t)
             h_squares = stage.tile([P, MEM], BF16, name="h_squares%d" % t, tag="h_squares")
             nc.scalar.activation(
-                out=h_squares[:], in_=c_tiles[t][:, 0:MEM], func=ACT.Square, accum_out=stats[t][:, 0:1]
+                out=h_squares[:], in_=inputs[t][:, 0:MEM], func=ACT.Square, accum_out=stats[t][:, 0:1]
             )
 
         def quantise(t, half):
@@ -182,20 +192,26 @@ def tile_liquidmemorycell_pb_kernel(
             update[t] = stage.tile([P, MEM], F32, name="update%d" % t, tag="update")
             nc.scalar.activation(out=update[t][:], in_=logits[t][:, MEM:GATES], func=ACT.Sigmoid)
 
-        def mix(t):
+        def blend_kept(t):
             kept[t] = stage.tile([P, MEM], F32, name="kept%d" % t, tag="kept")
             nc.vector.scalar_tensor_tensor(
-                out=kept[t][:], in0=shifted[t][:], scalar=S_OFFSET, in1=c_tiles[t][:, 0:MEM],
+                out=kept[t][:], in0=shifted[t][:], scalar=S_OFFSET, in1=inputs[t][:, 0:MEM],
                 op0=ALU.add, op1=ALU.mult,
             )
-            change = stage.tile([P, MEM], F32, name="change%d" % t, tag="change")
+
+        def blend_change(t):
+            change[t] = stage.tile([P, MEM], F32, name="change%d" % t, tag="change")
             nc.vector.scalar_tensor_tensor(
-                out=change[:], in0=candidate[:, t, :], scalar=M_GAIN, in1=kept[t][:],
+                out=change[t][:], in0=inputs[t][:, DIN : DIN + MEM], scalar=M_GAIN, in1=kept[t][:],
                 op0=ALU.mult, op1=ALU.subtract,
             )
-            nc.vector.tensor_tensor(out=change[:], in0=change[:], in1=update[t][:], op=ALU.mult)
+
+        def blend_gate(t):
+            nc.vector.tensor_tensor(out=change[t][:], in0=change[t][:], in1=update[t][:], op=ALU.mult)
+
+        def blend_sum(t):
             blend[t] = stage.tile([P, MEM], F32, name="blend%d" % t, tag="blend")
-            nc.vector.tensor_tensor(out=blend[t][:], in0=change[:], in1=kept[t][:], op=ALU.add)
+            nc.vector.tensor_tensor(out=blend[t][:], in0=change[t][:], in1=kept[t][:], op=ALU.add)
 
         def square_m(t):
             m_squares = stage.tile([P, MEM], BF16, name="m_squares%d" % t, tag="m_squares")
@@ -208,40 +224,58 @@ def tile_liquidmemorycell_pb_kernel(
             nc.gpsimd.tensor_tensor(out=scale[t][:], in0=floored[:], in1=powers[:], op=ALU.pow)
 
         def finish(t):
-            result = keep.tile([P, MEM], F32, name="result%d" % t)
+            result = leaving.tile([P, MEM], F32, name="result%d" % t, tag="result")
             nc.vector.tensor_scalar(
                 out=result[:], in0=blend[t][:], scalar1=scale[t][:, 0:1], scalar2=scale[t][:, 1:2],
                 op0=ALU.mult, op1=ALU.mult,
             )
-            nc.sync.dma_start(out=out_rows[:, t, :], in_=result[:])
+            nc.sync.dma_start(out=out[t * P : (t + 1) * P, :], in_=result[:])
 
         def live(t):
             return 0 <= t < TILES
 
-        for ahead in range(TILES + 3):
-            if live(ahead):
-                transpose(ahead)
-            if live(ahead - 2):
-                add_bias(ahead - 2)
-            if live(ahead - 3):
-                finish(ahead - 3)
-            if live(ahead):
-                copy_out(ahead, 0)
-            if live(ahead - 2):
-                gates(ahead - 2)
-            if live(ahead):
+        def step(now):
+            if live(now):
+                transpose(now)
+            if live(now - 2):
+                add_bias(now - 2)
+            if live(now - 3):
+                norms(now - 3)
+            if live(now):
+                copy_out(now, 0)
+            if live(now - 2):
+                gates(now - 2)
+            if live(now + 1):
+                sort_on_vector(now + 1)
+            if live(now):
                 for j in range(1, BANKS):
-                    copy_out(ahead, j)
-                square_h(ahead)
-            if live(ahead - 2):
-                mix(ahead - 2)
-            if live(ahead):
-                quantise(ahead, 0)
-            if live(ahead - 2):
-                square_m(ahead - 2)
-            if live(ahead):
-                quantise(ahead, 1)
-            if live(ahead - 2):
-                norms(ahead - 2)
-            if live(ahead - 1):
-                multiply(ahead - 1)
+                    copy_out(now, j)
+            if live(now - 2):
+                blend_kept(now - 2)
+            if live(now - 3):
+                finish(now - 3)
+            if live(now - 2):
+                blend_change(now - 2)
+            if live(now):
+                quantise(now, 0)
+            if live(now - 2):
+                blend_gate(now - 2)
+            if live(now):
+                quantise(now, 1)
+            if live(now - 2):
+                blend_sum(now - 2)
+            if live(now + 1):
+                sort_on_scalar(now + 1)
+                square_h(now + 1)
+            if live(now - 2):
+                square_m(now - 2)
+            if live(now - 2) and live(now - 2 + INPUT_BUFS):
+                load_inputs(now - 2 + INPUT_BUFS)
+            if live(now - 1):
+                multiply(now - 1)
+
+        for now in range(-1, 2):
+            step(now)
+        spread_biases()
+        for now in range(2, TILES + 3):
+            step(now)

@@ -20,10 +20,10 @@ GATES = 2 * MEM
 TILES = ROWS // P
 K_PASS = 4 * P
 GROUPS = DIN // K_PASS
+WORDS = K_PASS // 2
 BANK_GROUPS = 2
 BANKS = GROUPS // BANK_GROUPS
 HALF_GROUPS = GROUPS // 2
-SCALAR_SORTS = 2
 INPUT_BUFS = 8
 
 FLOPS = 2 * ROWS * DIN * GATES
@@ -115,29 +115,18 @@ def tile_liquidmemorycell_pb_kernel(
             )
             nc.vector.tensor_copy(out=bias[:, MEM:GATES], in_=bias_sums[:, MEM:GATES])
 
-        in_order, banks, grouped, codes, c_scales, gate_sums = {}, {}, {}, {}, {}, {}
+        banks, grouped, codes, c_scales, gate_sums = {}, {}, {}, {}, {}
         stats, logits, shifted, update, kept, change, blend, scale = {}, {}, {}, {}, {}, {}, {}, {}
 
-        def sort_views(t):
-            as_loaded = inputs[t][:, 0:DIN].bitcast(F32).rearrange("p (g w u) -> p u g w", g=GROUPS, u=2)
-            return as_loaded, in_order[t][:].rearrange("p g u w -> p u g w")
-
-        def sort_on_vector(t):
-            in_order[t] = stage.tile([P, GROUPS, 2, P], F32, name="in_order%d" % t, tag="in_order")
-            as_loaded, target = sort_views(t)
-            nc.vector.tensor_copy(out=target[:, :, SCALAR_SORTS:, :], in_=as_loaded[:, :, SCALAR_SORTS:, :])
-
-        def sort_on_scalar(t):
-            as_loaded, target = sort_views(t)
-            nc.scalar.copy(out=target[:, :, 0:SCALAR_SORTS, :], in_=as_loaded[:, :, 0:SCALAR_SORTS, :])
-
         def transpose(t):
+            words = inputs[t][:, 0:DIN].bitcast(F32)
             for j in range(BANKS):
                 banks[t, j] = turned.tile([P, BANK_GROUPS, 2, P], F32, name="turned%d_%d" % (t, j), tag="turned")
                 for i in range(BANK_GROUPS):
+                    first = (BANK_GROUPS * j + i) * WORDS
                     for u in range(2):
                         nc.tensor.transpose(
-                            banks[t, j][:, i, u, :], in_order[t][:, BANK_GROUPS * j + i, u, :], identity[:]
+                            banks[t, j][:, i, u, :], words[:, first + u : first + WORDS : 2], identity[:]
                         )
 
         def copy_out(t, j):
@@ -240,42 +229,37 @@ def tile_liquidmemorycell_pb_kernel(
             if live(now - 2):
                 add_bias(now - 2)
             if live(now - 3):
-                norms(now - 3)
+                square_m(now - 3)
             if live(now):
-                copy_out(now, 0)
+                square_h(now)
             if live(now - 2):
                 gates(now - 2)
-            if live(now + 1):
-                sort_on_vector(now + 1)
             if live(now):
-                for j in range(1, BANKS):
+                for j in range(BANKS):
                     copy_out(now, j)
+            if live(now - 1):
+                quantise(now - 1, 1)
             if live(now - 2):
                 blend_kept(now - 2)
             if live(now - 3):
-                finish(now - 3)
+                norms(now - 3)
             if live(now - 2):
                 blend_change(now - 2)
-            if live(now):
-                quantise(now, 0)
+            if live(now - 4):
+                finish(now - 4)
             if live(now - 2):
                 blend_gate(now - 2)
             if live(now):
-                quantise(now, 1)
+                quantise(now, 0)
             if live(now - 2):
                 blend_sum(now - 2)
-            if live(now + 1):
-                sort_on_scalar(now + 1)
-                square_h(now + 1)
-            if live(now - 2):
-                square_m(now - 2)
             if live(now - 2) and live(now - 2 + INPUT_BUFS):
                 load_inputs(now - 2 + INPUT_BUFS)
             if live(now - 1):
                 multiply(now - 1)
 
-        for now in range(-1, 2):
+        for now in range(2):
             step(now)
         spread_biases()
-        for now in range(2, TILES + 3):
+        for now in range(2, TILES + 4):
             step(now)

@@ -24,6 +24,8 @@ WORDS = K_PASS // 2
 BANK_GROUPS = 2
 BANKS = GROUPS // BANK_GROUPS
 HALF_GROUPS = GROUPS // 2
+SORTED = 4
+UNSORTED = GROUPS - SORTED
 INPUT_BUFS = 8
 
 FLOPS = 2 * ROWS * DIN * GATES
@@ -115,19 +117,29 @@ def tile_liquidmemorycell_pb_kernel(
             )
             nc.vector.tensor_copy(out=bias[:, MEM:GATES], in_=bias_sums[:, MEM:GATES])
 
-        banks, grouped, codes, c_scales, gate_sums = {}, {}, {}, {}, {}
+        in_order, banks, grouped, codes, c_scales, gate_sums = {}, {}, {}, {}, {}, {}
         stats, logits, shifted, update, kept, change, blend, scale = {}, {}, {}, {}, {}, {}, {}, {}
+
+        def sort(t):
+            in_order[t] = stage.tile([P, SORTED, 2, P], F32, name="in_order%d" % t, tag="in_order")
+            as_loaded = inputs[t][:, UNSORTED * K_PASS : DIN].bitcast(F32)
+            nc.vector.tensor_copy(
+                out=in_order[t][:].rearrange("p g u w -> p u g w"),
+                in_=as_loaded.rearrange("p (g w u) -> p u g w", g=SORTED, u=2),
+            )
 
         def transpose(t):
             words = inputs[t][:, 0:DIN].bitcast(F32)
             for j in range(BANKS):
                 banks[t, j] = turned.tile([P, BANK_GROUPS, 2, P], F32, name="turned%d_%d" % (t, j), tag="turned")
                 for i in range(BANK_GROUPS):
-                    first = (BANK_GROUPS * j + i) * WORDS
+                    g = BANK_GROUPS * j + i
                     for u in range(2):
-                        nc.tensor.transpose(
-                            banks[t, j][:, i, u, :], words[:, first + u : first + WORDS : 2], identity[:]
-                        )
+                        if g < UNSORTED:
+                            columns = words[:, g * WORDS + u : (g + 1) * WORDS : 2]
+                        else:
+                            columns = in_order[t][:, g - UNSORTED, u, :]
+                        nc.tensor.transpose(banks[t, j][:, i, u, :], columns, identity[:])
 
         def copy_out(t, j):
             if j == 0:
@@ -243,6 +255,8 @@ def tile_liquidmemorycell_pb_kernel(
                 blend_kept(now - 2)
             if live(now - 3):
                 norms(now - 3)
+            if live(now + 1):
+                sort(now + 1)
             if live(now - 2):
                 blend_change(now - 2)
             if live(now - 4):
@@ -258,7 +272,7 @@ def tile_liquidmemorycell_pb_kernel(
             if live(now - 1):
                 multiply(now - 1)
 
-        for now in range(2):
+        for now in range(-1, 2):
             step(now)
         spread_biases()
         for now in range(2, TILES + 4):

@@ -75,35 +75,42 @@ def tile_liquidmemorycell_pb_kernel(
 
         inputs = {}
 
+        def live(t):
+            return 0 <= t < TILES
+
         def load_inputs(t):
-            rows = slice(t * P, (t + 1) * P)
-            inputs[t] = arrivals.tile([P, DIN + MEM], BF16, name="inputs%d" % t, tag="inputs")
-            nc.sync.dma_start(out=inputs[t][:, 0:MEM], in_=h[rows, :])
-            nc.sync.dma_start(out=inputs[t][:, MEM:DIN], in_=x[rows, :])
-            nc.sync.dma_start(out=inputs[t][:, DIN : DIN + MEM], in_=h_candidate[rows, :])
+            if live(t):
+                rows = slice(t * P, (t + 1) * P)
+                inputs[t] = arrivals.tile([P, DIN + MEM], BF16, name="inputs%d" % t, tag="inputs")
+                nc.sync.dma_start(out=inputs[t][:, 0:MEM], in_=h[rows, :])
+                nc.sync.dma_start(out=inputs[t][:, MEM:DIN], in_=x[rows, :])
+            if live(t - 2):
+                rows = slice((t - 2) * P, (t - 1) * P)
+                nc.sync.dma_start(out=inputs[t - 2][:, DIN : DIN + MEM], in_=h_candidate[rows, :])
 
         w_words = keep.tile([P, GROUPS, GATES], U32, name="w_words", align_bytes=64)
 
-        def load_weights():
-            for gate, scales in enumerate((Wd_scales, Wu_scales)):
-                cols = slice(gate * MEM, (gate + 1) * MEM)
-                for quadrant in range(4):
-                    nc.sync.dma_start(
-                        out=w_scales[32 * quadrant : 32 * quadrant + 4, :, cols].bitcast(I32),
-                        in_=scales[:, 4 * quadrant : 4 * quadrant + 4, :]
-                        .rearrange("g r n -> r g n")
-                        .bitcast(I32),
-                    )
-            for gate, words in enumerate((Wd_words, Wu_words)):
-                cols = slice(gate * MEM, (gate + 1) * MEM)
+        def load_scales(gate, scales):
+            cols = slice(gate * MEM, (gate + 1) * MEM)
+            for quadrant in range(4):
                 nc.sync.dma_start(
-                    out=w_words[:, :, cols].bitcast(I32),
-                    in_=words.rearrange("g p n i -> p g (n i)").bitcast(I32),
+                    out=w_scales[32 * quadrant : 32 * quadrant + 4, :, cols].bitcast(I32),
+                    in_=scales[:, 4 * quadrant : 4 * quadrant + 4, :].rearrange("g r n -> r g n").bitcast(I32),
                 )
 
+        def load_words(gate, words):
+            cols = slice(gate * MEM, (gate + 1) * MEM)
+            nc.sync.dma_start(
+                out=w_words[:, :, cols].bitcast(I32),
+                in_=words.rearrange("g p n i -> p g (n i)").bitcast(I32),
+            )
+
         load_inputs(0)
+        load_scales(0, Wd_scales)
         load_inputs(1)
-        load_weights()
+        load_scales(1, Wu_scales)
+        load_words(0, Wd_words)
+        load_words(1, Wu_words)
         for t in range(2, INPUT_BUFS):
             load_inputs(t)
 
@@ -232,9 +239,6 @@ def tile_liquidmemorycell_pb_kernel(
             )
             nc.sync.dma_start(out=out[t * P : (t + 1) * P, :], in_=result[:])
 
-        def live(t):
-            return 0 <= t < TILES
-
         def step(now):
             if live(now):
                 transpose(now)
@@ -267,7 +271,7 @@ def tile_liquidmemorycell_pb_kernel(
                 quantise(now, 0)
             if live(now - 2):
                 blend_sum(now - 2)
-            if live(now - 2) and live(now - 2 + INPUT_BUFS):
+            if live(now - 2):
                 load_inputs(now - 2 + INPUT_BUFS)
             if live(now - 1):
                 multiply(now - 1)

@@ -26,6 +26,8 @@ BANKS = GROUPS // BANK_GROUPS
 HALF_GROUPS = GROUPS // 2
 SORTED = 4
 UNSORTED = GROUPS - SORTED
+NORM_BATCHES = [(0, 4), (4, 8), (8, 12), (12, 14), (14, 15), (15, 16)]
+BATCH_MAX = 4
 INPUT_BUFS = 8
 
 FLOPS = 2 * ROWS * DIN * GATES
@@ -49,6 +51,7 @@ def tile_liquidmemorycell_pb_kernel(
         keep = stack.enter_context(tc.tile_pool(name="keep", bufs=1))
         arrivals = stack.enter_context(tc.tile_pool(name="arrivals", bufs=INPUT_BUFS))
         stage = stack.enter_context(tc.tile_pool(name="stage", bufs=2))
+        blends = stack.enter_context(tc.tile_pool(name="blends", bufs=8))
         leaving = stack.enter_context(tc.tile_pool(name="leaving", bufs=3))
         turned = stack.enter_context(tc.psum_pool(name="turned", bufs=6))
         sums = stack.enter_context(tc.psum_pool(name="sums", bufs=2))
@@ -59,19 +62,19 @@ def tile_liquidmemorycell_pb_kernel(
         nc.vector.memset(bias_row[:], 0.0)
         ones = keep.tile([P, P], BF16, name="ones")
         nc.vector.memset(ones[:], 1.0)
-        floors = keep.tile([P, 2], F32, name="floors")
-        nc.vector.memset(floors[:, 0:1], H_NORM_FLOOR * H_NORM_FLOOR)
-        nc.vector.memset(floors[:, 1:2], M_NORM_FLOOR * M_NORM_FLOOR)
-        powers = keep.tile([P, 2], F32, name="powers")
-        nc.vector.memset(powers[:, 0:1], 0.5)
-        nc.vector.memset(powers[:, 1:2], -0.5)
+        floors = keep.tile([P, 2, BATCH_MAX], F32, name="floors")
+        nc.vector.memset(floors[:, 0, :], H_NORM_FLOOR * H_NORM_FLOOR)
+        nc.vector.memset(floors[:, 1, :], M_NORM_FLOOR * M_NORM_FLOOR)
+        powers = keep.tile([P, 2, BATCH_MAX], F32, name="powers")
+        nc.vector.memset(powers[:, 0, :], 0.5)
+        nc.vector.memset(powers[:, 1, :], -0.5)
         identity = keep.tile([P, P], F32, name="identity")
         make_identity(nc, identity[:])
 
         nc.scalar.dma_start(out=bias_row[0:1, 0:MEM], in_=bd.unsqueeze(0))
         nc.scalar.dma_start(out=bias_row[0:1, MEM:GATES], in_=bu.unsqueeze(0))
         table_warmer = keep.tile([P, 1], F32, name="table_warmer")
-        nc.scalar.activation(out=table_warmer[:], in_=powers[:, 0:1], func=ACT.Sigmoid)
+        nc.scalar.activation(out=table_warmer[:], in_=powers[:, 0, 0:1], func=ACT.Sigmoid)
 
         inputs = {}
 
@@ -125,7 +128,13 @@ def tile_liquidmemorycell_pb_kernel(
             nc.vector.tensor_copy(out=bias[:, MEM:GATES], in_=bias_sums[:, MEM:GATES])
 
         in_order, banks, grouped, codes, c_scales, gate_sums = {}, {}, {}, {}, {}, {}
-        stats, logits, shifted, update, kept, change, blend, scale = {}, {}, {}, {}, {}, {}, {}, {}
+        logits, shifted, update, kept, change, blend, scale = {}, {}, {}, {}, {}, {}, {}
+        stats, batch_of, place_of = [], {}, {}
+        for b, (first, end) in enumerate(NORM_BATCHES):
+            stats.append(keep.tile([P, 2, end - first], F32, name="stats%d" % b))
+            for t in range(first, end):
+                batch_of[t], place_of[t] = b, t - first
+        waiting = []
 
         def sort(t):
             in_order[t] = stage.tile([P, SORTED, 2, P], F32, name="in_order%d" % t, tag="in_order")
@@ -158,10 +167,9 @@ def tile_liquidmemorycell_pb_kernel(
             )
 
         def square_h(t):
-            stats[t] = keep.tile([P, 2], F32, name="stats%d" % t)
             h_squares = stage.tile([P, MEM], BF16, name="h_squares%d" % t, tag="h_squares")
             nc.scalar.activation(
-                out=h_squares[:], in_=inputs[t][:, 0:MEM], func=ACT.Square, accum_out=stats[t][:, 0:1]
+                out=h_squares[:], in_=inputs[t][:, 0:MEM], func=ACT.Square, accum_out=stats[batch_of[t]][:, 0, place_of[t] : place_of[t] + 1]
             )
 
         def quantise(t, half):
@@ -218,28 +226,37 @@ def tile_liquidmemorycell_pb_kernel(
             nc.vector.tensor_tensor(out=change[t][:], in0=change[t][:], in1=update[t][:], op=ALU.mult)
 
         def blend_sum(t):
-            blend[t] = stage.tile([P, MEM], F32, name="blend%d" % t, tag="blend")
+            blend[t] = blends.tile([P, MEM], F32, name="blend%d" % t, tag="blend")
             nc.vector.tensor_tensor(out=blend[t][:], in0=change[t][:], in1=kept[t][:], op=ALU.add)
 
         def square_m(t):
             m_squares = stage.tile([P, MEM], BF16, name="m_squares%d" % t, tag="m_squares")
-            nc.scalar.activation(out=m_squares[:], in_=blend[t][:], func=ACT.Square, accum_out=stats[t][:, 1:2])
+            nc.scalar.activation(out=m_squares[:], in_=blend[t][:], func=ACT.Square,
+                                 accum_out=stats[batch_of[t]][:, 1, place_of[t] : place_of[t] + 1])
 
         def norms(t):
-            floored = keep.tile([P, 2], F32, name="floored%d" % t)
-            nc.vector.tensor_tensor(out=floored[:], in0=stats[t][:], in1=floors[:], op=ALU.max)
-            scale[t] = keep.tile([P, 2], F32, name="scale%d" % t)
-            nc.gpsimd.tensor_tensor(out=scale[t][:], in0=floored[:], in1=powers[:], op=ALU.pow)
+            b = batch_of[t]
+            first, end = NORM_BATCHES[b]
+            if t + 1 < end:
+                return
+            floored = keep.tile([P, 2, end - first], F32, name="floored%d" % b)
+            nc.vector.tensor_tensor(out=floored[:], in0=stats[b][:], in1=floors[:, :, 0 : end - first], op=ALU.max)
+            scale[b] = keep.tile([P, 2, end - first], F32, name="scale%d" % b)
+            nc.gpsimd.tensor_tensor(out=scale[b][:], in0=floored[:], in1=powers[:, :, 0 : end - first], op=ALU.pow)
+            waiting.extend(range(first, end))
 
         def finish(t):
+            b, i = batch_of[t], place_of[t]
             result = leaving.tile([P, MEM], F32, name="result%d" % t, tag="result")
             nc.vector.tensor_scalar(
-                out=result[:], in0=blend[t][:], scalar1=scale[t][:, 0:1], scalar2=scale[t][:, 1:2],
+                out=result[:], in0=blend[t][:], scalar1=scale[b][:, 0, i : i + 1], scalar2=scale[b][:, 1, i : i + 1],
                 op0=ALU.mult, op1=ALU.mult,
             )
             nc.sync.dma_start(out=out[t * P : (t + 1) * P, :], in_=result[:])
 
         def step(now):
+            ready = waiting[0 : 1 if now < TILES else TILES]
+            waiting[0:len(ready)] = []
             if live(now):
                 transpose(now)
             if live(now - 2):
@@ -263,8 +280,8 @@ def tile_liquidmemorycell_pb_kernel(
                 sort(now + 1)
             if live(now - 2):
                 blend_change(now - 2)
-            if live(now - 4):
-                finish(now - 4)
+            for t in ready:
+                finish(t)
             if live(now - 2):
                 blend_gate(now - 2)
             if live(now):

@@ -52,7 +52,7 @@ def tile_liquidmemorycell_pb_kernel(
         arrivals = stack.enter_context(tc.tile_pool(name="arrivals", bufs=INPUT_BUFS))
         stage = stack.enter_context(tc.tile_pool(name="stage", bufs=2))
         blends = stack.enter_context(tc.tile_pool(name="blends", bufs=8))
-        leaving = stack.enter_context(tc.tile_pool(name="leaving", bufs=3))
+        leaving = stack.enter_context(tc.tile_pool(name="leaving", bufs=8))
         turned = stack.enter_context(tc.psum_pool(name="turned", bufs=6))
         sums = stack.enter_context(tc.psum_pool(name="sums", bufs=2))
 
@@ -71,8 +71,6 @@ def tile_liquidmemorycell_pb_kernel(
         identity = keep.tile([P, P], F32, name="identity")
         make_identity(nc, identity[:])
 
-        nc.scalar.dma_start(out=bias_row[0:1, 0:MEM], in_=bd.unsqueeze(0))
-        nc.scalar.dma_start(out=bias_row[0:1, MEM:GATES], in_=bu.unsqueeze(0))
         table_warmer = keep.tile([P, 1], F32, name="table_warmer")
         nc.scalar.activation(out=table_warmer[:], in_=powers[:, 0, 0:1], func=ACT.Sigmoid)
 
@@ -81,12 +79,13 @@ def tile_liquidmemorycell_pb_kernel(
         def live(t):
             return 0 <= t < TILES
 
-        def load_inputs(t):
+        def load_inputs(t, cuts=(MEM, DIN)):
             if live(t):
                 rows = slice(t * P, (t + 1) * P)
                 inputs[t] = arrivals.tile([P, DIN + MEM], BF16, name="inputs%d" % t, tag="inputs")
                 nc.sync.dma_start(out=inputs[t][:, 0:MEM], in_=h[rows, :])
-                nc.sync.dma_start(out=inputs[t][:, MEM:DIN], in_=x[rows, :])
+                for a, b in zip(cuts[:-1], cuts[1:]):
+                    nc.sync.dma_start(out=inputs[t][:, a:b], in_=x[rows, a - MEM : b - MEM])
             if live(t - 2):
                 rows = slice((t - 2) * P, (t - 1) * P)
                 nc.sync.dma_start(out=inputs[t - 2][:, DIN : DIN + MEM], in_=h_candidate[rows, :])
@@ -101,19 +100,24 @@ def tile_liquidmemorycell_pb_kernel(
                     in_=scales[:, 4 * quadrant : 4 * quadrant + 4, :].rearrange("g r n -> r g n").bitcast(I32),
                 )
 
-        def load_words(gate, words):
+        def load_words(gate, words, groups):
             cols = slice(gate * MEM, (gate + 1) * MEM)
             nc.sync.dma_start(
-                out=w_words[:, :, cols].bitcast(I32),
-                in_=words.rearrange("g p n i -> p g (n i)").bitcast(I32),
+                out=w_words[:, groups, cols].bitcast(I32),
+                in_=words[groups].rearrange("g p n i -> p g (n i)").bitcast(I32),
             )
 
-        load_inputs(0)
+        load_inputs(0, (MEM, DIN // 2, DIN))
         load_scales(0, Wd_scales)
         load_inputs(1)
+        nc.scalar.dma_start(out=bias_row[0:1, 0:MEM], in_=bd.unsqueeze(0))
+        nc.scalar.dma_start(out=bias_row[0:1, MEM:GATES], in_=bu.unsqueeze(0))
+        first_half, last_half = slice(0, HALF_GROUPS), slice(HALF_GROUPS, GROUPS)
+        load_words(0, Wd_words, first_half)
+        load_words(1, Wu_words, first_half)
         load_scales(1, Wu_scales)
-        load_words(0, Wd_words)
-        load_words(1, Wu_words)
+        load_words(0, Wd_words, last_half)
+        load_words(1, Wu_words, last_half)
         for t in range(2, INPUT_BUFS):
             load_inputs(t)
 
@@ -134,6 +138,7 @@ def tile_liquidmemorycell_pb_kernel(
             stats.append(keep.tile([P, 2, end - first], F32, name="stats%d" % b))
             for t in range(first, end):
                 batch_of[t], place_of[t] = b, t - first
+        powered = {}
         waiting = []
 
         def sort(t):
@@ -157,11 +162,11 @@ def tile_liquidmemorycell_pb_kernel(
                             columns = in_order[t][:, g - UNSORTED, u, :]
                         nc.tensor.transpose(banks[t, j][:, i, u, :], columns, identity[:])
 
-        def copy_out(t, j):
+        def copy_out(t, j, copy=nc.scalar.copy):
             if j == 0:
                 grouped[t] = stage.tile([P, DIN], BF16, name="grouped%d" % t, tag="grouped", align_bytes=64)
             pairs = grouped[t][:].bitcast(F32).rearrange("p (g r u) -> p g r u", g=GROUPS, u=2)
-            nc.scalar.copy(
+            copy(
                 out=pairs[:, BANK_GROUPS * j : BANK_GROUPS * (j + 1), :, :],
                 in_=banks[t, j][:].rearrange("p g u r -> p g r u"),
             )
@@ -186,14 +191,17 @@ def tile_liquidmemorycell_pb_kernel(
 
         def multiply(t):
             gate_sums[t] = sums.tile([P, GATES], F32, name="gate_sums%d" % t, tag="sums")
+            multiply_into(t, gate_sums[t][:], slice(0, GATES))
+
+        def multiply_into(t, out, columns):
             for g in range(GROUPS):
                 rows = slice(g * P, (g + 1) * P)
                 nc.tensor.matmul_mx(
-                    out=gate_sums[t][:],
+                    out=out,
                     lhsT=codes[t][:, rows].bitcast(FP8X4),
                     lhsT_scale=c_scales[t][:, rows],
-                    rhs=w_words[:, g, :].bitcast(FP8X4),
-                    rhs_scale=w_scales[:, g, :],
+                    rhs=w_words[:, g, columns].bitcast(FP8X4),
+                    rhs_scale=w_scales[:, g, columns],
                     start=(g == 0),
                     stop=(g == GROUPS - 1),
                 )
@@ -202,11 +210,28 @@ def tile_liquidmemorycell_pb_kernel(
             logits[t] = stage.tile([P, GATES], F32, name="logits%d" % t, tag="logits")
             nc.vector.tensor_tensor(out=logits[t][:], in0=gate_sums[t][:], in1=bias[:], op=ALU.add)
 
-        def gates(t):
+        D_COLS, U_COLS = slice(0, MEM), slice(MEM, GATES)
+
+        def decay_gate(t):
             shifted[t] = stage.tile([P, MEM], F32, name="shifted%d" % t, tag="shifted")
-            nc.scalar.activation(out=shifted[t][:], in_=logits[t][:, 0:MEM], func=ACT.Sigmoid, scale=-1.0)
+            nc.scalar.activation(out=shifted[t][:], in_=logits[t][:, D_COLS], func=ACT.Sigmoid, scale=-1.0)
+
+        def update_gate(t):
             update[t] = stage.tile([P, MEM], F32, name="update%d" % t, tag="update")
-            nc.scalar.activation(out=update[t][:], in_=logits[t][:, MEM:GATES], func=ACT.Sigmoid)
+            nc.scalar.activation(out=update[t][:], in_=logits[t][:, U_COLS], func=ACT.Sigmoid)
+
+        def multiply_gate(t, columns):
+            gate_sums[t, columns.start] = sums.tile(
+                [P, MEM], F32, name="gate_sums%d_%d" % (t, columns.start), tag="sums"
+            )
+            multiply_into(t, gate_sums[t, columns.start][:], columns)
+
+        def add_one_bias(t, columns):
+            if columns.start == 0:
+                logits[t] = stage.tile([P, GATES], F32, name="logits%d" % t, tag="logits")
+            nc.vector.tensor_tensor(
+                out=logits[t][:, columns], in0=gate_sums[t, columns.start][:], in1=bias[:, columns], op=ALU.add
+            )
 
         def blend_kept(t):
             kept[t] = stage.tile([P, MEM], F32, name="kept%d" % t, tag="kept")
@@ -241,22 +266,32 @@ def tile_liquidmemorycell_pb_kernel(
                 return
             floored = keep.tile([P, 2, end - first], F32, name="floored%d" % b)
             nc.vector.tensor_tensor(out=floored[:], in0=stats[b][:], in1=floors[:, :, 0 : end - first], op=ALU.max)
-            scale[b] = keep.tile([P, 2, end - first], F32, name="scale%d" % b)
-            nc.gpsimd.tensor_tensor(out=scale[b][:], in0=floored[:], in1=powers[:, :, 0 : end - first], op=ALU.pow)
+            powered[b] = keep.tile([P, 2, end - first], F32, name="powered%d" % b)
+            nc.gpsimd.tensor_tensor(out=powered[b][:], in0=floored[:], in1=powers[:, :, 0 : end - first], op=ALU.pow)
+            if end < TILES:
+                scale[b] = keep.tile([P, end - first], F32, name="scale%d" % b)
+                nc.gpsimd.tensor_tensor(
+                    out=scale[b][:], in0=powered[b][:, 0, :], in1=powered[b][:, 1, :], op=ALU.mult
+                )
             waiting.extend(range(first, end))
 
         def finish(t):
             b, i = batch_of[t], place_of[t]
             result = leaving.tile([P, MEM], F32, name="result%d" % t, tag="result")
-            nc.vector.tensor_scalar(
-                out=result[:], in0=blend[t][:], scalar1=scale[b][:, 0, i : i + 1], scalar2=scale[b][:, 1, i : i + 1],
-                op0=ALU.mult, op1=ALU.mult,
-            )
+            if t + 1 < TILES:
+                nc.scalar.activation(out=result[:], in_=blend[t][:], func=ACT.Copy, scale=scale[b][:, i : i + 1])
+            else:
+                nc.vector.tensor_scalar(
+                    out=result[:], in0=blend[t][:], scalar1=powered[b][:, 0, i : i + 1],
+                    scalar2=powered[b][:, 1, i : i + 1], op0=ALU.mult, op1=ALU.mult,
+                )
             nc.sync.dma_start(out=out[t * P : (t + 1) * P, :], in_=result[:])
 
         def step(now):
-            ready = waiting[0 : 1 if now < TILES else TILES]
+            ready = waiting[0:1]
             waiting[0:len(ready)] = []
+            if now == 2:
+                multiply(1)
             if live(now):
                 transpose(now)
             if live(now - 2):
@@ -266,35 +301,90 @@ def tile_liquidmemorycell_pb_kernel(
             if live(now):
                 square_h(now)
             if live(now - 2):
-                gates(now - 2)
+                decay_gate(now - 2)
+                update_gate(now - 2)
             if live(now):
                 for j in range(BANKS):
                     copy_out(now, j)
-            if live(now - 1):
+            for t in ready:
+                finish(t)
+            if live(now - 1) and now != 2:
                 quantise(now - 1, 1)
             if live(now - 2):
                 blend_kept(now - 2)
             if live(now - 3):
                 norms(now - 3)
-            if live(now + 1):
+            if live(now + 1) and now >= 2:
                 sort(now + 1)
             if live(now - 2):
                 blend_change(now - 2)
-            for t in ready:
-                finish(t)
             if live(now - 2):
                 blend_gate(now - 2)
             if live(now):
                 quantise(now, 0)
+            if now == 1:
+                quantise(1, 1)
             if live(now - 2):
                 blend_sum(now - 2)
             if live(now - 2):
                 load_inputs(now - 2 + INPUT_BUFS)
-            if live(now - 1):
+            if now == 1:
+                spread_biases()
+            if live(now + 1) and now < 2:
+                sort(now + 1)
+            if live(now - 1) and now != 2:
                 multiply(now - 1)
 
-        for now in range(-1, 2):
+        for now in range(-1, TILES - 1):
             step(now)
-        spread_biases()
-        for now in range(2, TILES + 4):
-            step(now)
+
+        a, b, c = TILES - 3, TILES - 2, TILES - 1
+
+        def finish_waiting(count):
+            for t in waiting[0:count]:
+                finish(t)
+            waiting[0:count] = []
+
+        transpose(c)
+        square_m(a - 1)
+        square_h(c)
+        add_bias(a)
+        decay_gate(a)
+        update_gate(a)
+        for j in range(BANKS):
+            copy_out(c, j)
+        quantise(b, 1)
+        multiply(b)
+        blend_kept(a)
+        blend_change(a)
+        blend_gate(a)
+        quantise(c, 0)
+        blend_sum(a)
+        quantise(c, 1)
+        multiply_gate(c, D_COLS)
+        square_m(a)
+        add_bias(b)
+        multiply_gate(c, U_COLS)
+        decay_gate(b)
+        update_gate(b)
+        norms(a)
+        blend_kept(b)
+        blend_change(b)
+        finish_waiting(1)
+        add_one_bias(c, D_COLS)
+        decay_gate(c)
+        blend_gate(b)
+        blend_kept(c)
+        blend_sum(b)
+        blend_change(c)
+        square_m(b)
+        add_one_bias(c, U_COLS)
+        update_gate(c)
+        norms(b)
+        finish_waiting(1)
+        blend_gate(c)
+        blend_sum(c)
+        finish_waiting(1)
+        square_m(c)
+        norms(c)
+        finish_waiting(TILES)

@@ -50,7 +50,7 @@ def tile_liquidmemorycell_pb_kernel(
         stack.enter_context(tc.manual_schedule())
         keep = stack.enter_context(tc.tile_pool(name="keep", bufs=1))
         arrivals = stack.enter_context(tc.tile_pool(name="arrivals", bufs=INPUT_BUFS))
-        stage = stack.enter_context(tc.tile_pool(name="stage", bufs=2))
+        stage = stack.enter_context(tc.tile_pool(name="stage", bufs=3))
         blends = stack.enter_context(tc.tile_pool(name="blends", bufs=8))
         leaving = stack.enter_context(tc.tile_pool(name="leaving", bufs=8))
         turned = stack.enter_context(tc.psum_pool(name="turned", bufs=6))
@@ -294,38 +294,40 @@ def tile_liquidmemorycell_pb_kernel(
                 multiply(1)
             if live(now):
                 transpose(now)
+                square_h(now)
+            if live(now - 1) and now != 2:
+                quantise(now - 1, 1)
+            if live(now - 3):
+                blend_gate(now - 3)
             if live(now - 2):
                 add_bias(now - 2)
             if live(now - 3):
-                square_m(now - 3)
+                blend_sum(now - 3)
             if live(now):
-                square_h(now)
+                copy_out(now, 0)
+                copy_out(now, 1)
             if live(now - 2):
                 decay_gate(now - 2)
                 update_gate(now - 2)
-            if live(now):
-                for j in range(BANKS):
-                    copy_out(now, j)
-            for t in ready:
-                finish(t)
-            if live(now - 1) and now != 2:
-                quantise(now - 1, 1)
-            if live(now - 2):
-                blend_kept(now - 2)
             if live(now - 3):
-                norms(now - 3)
+                square_m(now - 3)
+            if live(now):
+                copy_out(now, 2)
+                copy_out(now, 3)
             if live(now + 1) and now >= 2:
                 sort(now + 1)
             if live(now - 2):
-                blend_change(now - 2)
-            if live(now - 2):
-                blend_gate(now - 2)
+                blend_kept(now - 2)
             if live(now):
                 quantise(now, 0)
             if now == 1:
                 quantise(1, 1)
             if live(now - 2):
-                blend_sum(now - 2)
+                blend_change(now - 2)
+            if live(now - 3):
+                norms(now - 3)
+            for t in ready:
+                finish(t)
             if live(now - 2):
                 load_inputs(now - 2 + INPUT_BUFS)
             if now == 1:
@@ -346,33 +348,37 @@ def tile_liquidmemorycell_pb_kernel(
             waiting[0:count] = []
 
         transpose(c)
-        square_m(a - 1)
         square_h(c)
-        add_bias(a)
-        decay_gate(a)
-        update_gate(a)
-        for j in range(BANKS):
-            copy_out(c, j)
         quantise(b, 1)
         multiply(b)
+        blend_gate(a - 1)
+        add_bias(a)
+        blend_sum(a - 1)
+        copy_out(c, 0)
+        copy_out(c, 1)
+        decay_gate(a)
+        update_gate(a)
+        copy_out(c, 2)
+        copy_out(c, 3)
+        square_m(a - 1)
         blend_kept(a)
-        blend_change(a)
-        blend_gate(a)
         quantise(c, 0)
-        blend_sum(a)
+        blend_change(a)
         quantise(c, 1)
         multiply_gate(c, D_COLS)
-        square_m(a)
+        blend_gate(a)
         add_bias(b)
         multiply_gate(c, U_COLS)
+        blend_sum(a)
         decay_gate(b)
         update_gate(b)
-        norms(a)
+        square_m(a)
         blend_kept(b)
-        blend_change(b)
         finish_waiting(1)
         add_one_bias(c, D_COLS)
         decay_gate(c)
+        blend_change(b)
+        norms(a)
         blend_gate(b)
         blend_kept(c)
         blend_sum(b)
@@ -381,10 +387,9 @@ def tile_liquidmemorycell_pb_kernel(
         add_one_bias(c, U_COLS)
         update_gate(c)
         norms(b)
-        finish_waiting(1)
+        finish_waiting(2)
         blend_gate(c)
         blend_sum(c)
-        finish_waiting(1)
         square_m(c)
         norms(c)
         finish_waiting(TILES)

@@ -24,7 +24,7 @@ WORDS = K_PASS // 2
 BANK_GROUPS = 2
 BANKS = GROUPS // BANK_GROUPS
 HALF_GROUPS = GROUPS // 2
-SORTED = 4
+SORTED = 6
 UNSORTED = GROUPS - SORTED
 NORM_BATCHES = [(0, 4), (4, 8), (8, 12), (12, 14), (14, 15), (15, 16)]
 BATCH_MAX = 4
@@ -156,7 +156,7 @@ def tile_liquidmemorycell_pb_kernel(
                 for i in range(BANK_GROUPS):
                     g = BANK_GROUPS * j + i
                     for u in range(2):
-                        if g < UNSORTED:
+                        if t == 0 or g < UNSORTED:
                             columns = words[:, g * WORDS + u : (g + 1) * WORDS : 2]
                         else:
                             columns = in_order[t][:, g - UNSORTED, u, :]
@@ -332,7 +332,7 @@ def tile_liquidmemorycell_pb_kernel(
                 load_inputs(now - 2 + INPUT_BUFS)
             if now == 1:
                 spread_biases()
-            if live(now + 1) and now < 2:
+            if now in (0, 1):
                 sort(now + 1)
             if live(now - 1) and now != 2:
                 multiply(now - 1)

@@ -24,10 +24,10 @@ WORDS = K_PASS // 2
 BANK_GROUPS = 2
 BANKS = GROUPS // BANK_GROUPS
 HALF_GROUPS = GROUPS // 2
-SORTED = 6
+SORTED = 5
 UNSORTED = GROUPS - SORTED
-NORM_BATCHES = [(0, 4), (4, 8), (8, 12), (12, 14), (14, 15), (15, 16)]
-BATCH_MAX = 4
+NORM_BATCHES = [(0, 2), (2, 4), (4, 6), (6, 8), (8, 10), (10, 12), (12, 14), (14, 16)]
+BATCH_MAX = 2
 INPUT_BUFS = 8
 
 FLOPS = 2 * ROWS * DIN * GATES
@@ -51,7 +51,7 @@ def tile_liquidmemorycell_pb_kernel(
         keep = stack.enter_context(tc.tile_pool(name="keep", bufs=1))
         arrivals = stack.enter_context(tc.tile_pool(name="arrivals", bufs=INPUT_BUFS))
         stage = stack.enter_context(tc.tile_pool(name="stage", bufs=3))
-        blends = stack.enter_context(tc.tile_pool(name="blends", bufs=8))
+        blends = stack.enter_context(tc.tile_pool(name="blends", bufs=10))
         leaving = stack.enter_context(tc.tile_pool(name="leaving", bufs=8))
         turned = stack.enter_context(tc.psum_pool(name="turned", bufs=6))
         sums = stack.enter_context(tc.psum_pool(name="sums", bufs=2))
@@ -139,7 +139,6 @@ def tile_liquidmemorycell_pb_kernel(
             for t in range(first, end):
                 batch_of[t], place_of[t] = b, t - first
         powered = {}
-        waiting = []
 
         def sort(t):
             in_order[t] = stage.tile([P, SORTED, 2, P], F32, name="in_order%d" % t, tag="in_order")
@@ -177,16 +176,15 @@ def tile_liquidmemorycell_pb_kernel(
                 out=h_squares[:], in_=inputs[t][:, 0:MEM], func=ACT.Square, accum_out=stats[batch_of[t]][:, 0, place_of[t] : place_of[t] + 1]
             )
 
-        def quantise(t, half):
-            if half == 0:
+        def quantise(t, first, end):
+            if first == 0:
                 codes[t] = stage.tile([P, GROUPS * P], U32, name="codes%d" % t, tag="codes", align_bytes=64)
                 c_scales[t] = stage.tile([P, GROUPS * P], U8, name="c_scales%d" % t, tag="c_scales", align_bytes=64)
-            width = HALF_GROUPS * P
-            cols = slice(half * width, (half + 1) * width)
+            cols = slice(first * P, end * P)
             nc.vector.quantize_mx(
                 out=codes[t][:, cols].bitcast(FP8X4),
                 scales=c_scales[t][:, cols],
-                in_=grouped[t][:, 4 * half * width : 4 * (half + 1) * width],
+                in_=grouped[t][:, first * K_PASS : end * K_PASS],
             )
 
         def multiply(t):
@@ -273,12 +271,14 @@ def tile_liquidmemorycell_pb_kernel(
                 nc.gpsimd.tensor_tensor(
                     out=scale[b][:], in0=powered[b][:, 0, :], in1=powered[b][:, 1, :], op=ALU.mult
                 )
-            waiting.extend(range(first, end))
+
+        def end_of(t):
+            return NORM_BATCHES[batch_of[t]][1]
 
         def finish(t):
             b, i = batch_of[t], place_of[t]
             result = leaving.tile([P, MEM], F32, name="result%d" % t, tag="result")
-            if t + 1 < TILES:
+            if end_of(t) < TILES:
                 nc.scalar.activation(out=result[:], in_=blend[t][:], func=ACT.Copy, scale=scale[b][:, i : i + 1])
             else:
                 nc.vector.tensor_scalar(
@@ -288,46 +288,45 @@ def tile_liquidmemorycell_pb_kernel(
             nc.sync.dma_start(out=out[t * P : (t + 1) * P, :], in_=result[:])
 
         def step(now):
-            ready = waiting[0:1]
-            waiting[0:len(ready)] = []
             if now == 2:
                 multiply(1)
             if live(now):
                 transpose(now)
+            if live(now - 4):
+                square_m(now - 4)
+            if live(now):
                 square_h(now)
             if live(now - 1) and now != 2:
-                quantise(now - 1, 1)
+                quantise(now - 1, HALF_GROUPS, GROUPS)
             if live(now - 3):
                 blend_gate(now - 3)
             if live(now - 2):
                 add_bias(now - 2)
             if live(now - 3):
                 blend_sum(now - 3)
+            if live(now - 4):
+                norms(now - 4)
             if live(now):
                 copy_out(now, 0)
                 copy_out(now, 1)
             if live(now - 2):
                 decay_gate(now - 2)
                 update_gate(now - 2)
-            if live(now - 3):
-                square_m(now - 3)
             if live(now):
                 copy_out(now, 2)
                 copy_out(now, 3)
+            if live(now - 5):
+                finish(now - 5)
             if live(now + 1) and now >= 2:
                 sort(now + 1)
             if live(now - 2):
                 blend_kept(now - 2)
             if live(now):
-                quantise(now, 0)
+                quantise(now, 0, HALF_GROUPS)
             if now == 1:
-                quantise(1, 1)
+                quantise(1, HALF_GROUPS, GROUPS)
             if live(now - 2):
                 blend_change(now - 2)
-            if live(now - 3):
-                norms(now - 3)
-            for t in ready:
-                finish(t)
             if live(now - 2):
                 load_inputs(now - 2 + INPUT_BUFS)
             if now == 1:
@@ -342,54 +341,52 @@ def tile_liquidmemorycell_pb_kernel(
 
         a, b, c = TILES - 3, TILES - 2, TILES - 1
 
-        def finish_waiting(count):
-            for t in waiting[0:count]:
-                finish(t)
-            waiting[0:count] = []
-
         transpose(c)
+        square_m(a - 2)
         square_h(c)
-        quantise(b, 1)
+        quantise(b, HALF_GROUPS, GROUPS)
         multiply(b)
         blend_gate(a - 1)
         add_bias(a)
         blend_sum(a - 1)
-        copy_out(c, 0)
-        copy_out(c, 1)
+        norms(a - 2)
+        for j in range(BANKS):
+            copy_out(c, j)
         decay_gate(a)
         update_gate(a)
-        copy_out(c, 2)
-        copy_out(c, 3)
         square_m(a - 1)
-        blend_kept(a)
-        quantise(c, 0)
-        blend_change(a)
-        quantise(c, 1)
+        finish(a - 3)
+        quantise(c, 0, HALF_GROUPS)
+        quantise(c, HALF_GROUPS, HALF_GROUPS + BANK_GROUPS)
+        quantise(c, HALF_GROUPS + BANK_GROUPS, GROUPS)
         multiply_gate(c, D_COLS)
-        blend_gate(a)
+        blend_kept(a)
         add_bias(b)
         multiply_gate(c, U_COLS)
-        blend_sum(a)
+        blend_change(a)
+        finish(a - 2)
         decay_gate(b)
         update_gate(b)
-        square_m(a)
-        blend_kept(b)
-        finish_waiting(1)
         add_one_bias(c, D_COLS)
         decay_gate(c)
-        blend_change(b)
-        norms(a)
-        blend_gate(b)
-        blend_kept(c)
-        blend_sum(b)
-        blend_change(c)
-        square_m(b)
+        blend_gate(a)
+        blend_kept(b)
+        blend_sum(a)
+        square_m(a)
         add_one_bias(c, U_COLS)
         update_gate(c)
-        norms(b)
-        finish_waiting(2)
+        blend_kept(c)
+        blend_change(b)
+        blend_change(c)
+        norms(a)
+        blend_gate(b)
         blend_gate(c)
+        blend_sum(b)
         blend_sum(c)
+        square_m(b)
         square_m(c)
         norms(c)
-        finish_waiting(TILES)
+        finish(a - 1)
+        finish(a)
+        finish(b)
+        finish(c)

@@ -51,7 +51,7 @@ def tile_liquidmemorycell_pb_kernel(
         keep = stack.enter_context(tc.tile_pool(name="keep", bufs=1))
         arrivals = stack.enter_context(tc.tile_pool(name="arrivals", bufs=INPUT_BUFS))
         stage = stack.enter_context(tc.tile_pool(name="stage", bufs=3))
-        blends = stack.enter_context(tc.tile_pool(name="blends", bufs=10))
+        blends = stack.enter_context(tc.tile_pool(name="blends", bufs=9))
         leaving = stack.enter_context(tc.tile_pool(name="leaving", bufs=8))
         turned = stack.enter_context(tc.psum_pool(name="turned", bufs=6))
         sums = stack.enter_context(tc.psum_pool(name="sums", bufs=2))
@@ -315,8 +315,8 @@ def tile_liquidmemorycell_pb_kernel(
             if live(now):
                 copy_out(now, 2)
                 copy_out(now, 3)
-            if live(now - 5):
-                finish(now - 5)
+            if live(now - 7):
+                finish(now - 7)
             if live(now + 1) and now >= 2:
                 sort(now + 1)
             if live(now - 2):
@@ -355,7 +355,7 @@ def tile_liquidmemorycell_pb_kernel(
         decay_gate(a)
         update_gate(a)
         square_m(a - 1)
-        finish(a - 3)
+        finish(a - 5)
         quantise(c, 0, HALF_GROUPS)
         quantise(c, HALF_GROUPS, HALF_GROUPS + BANK_GROUPS)
         quantise(c, HALF_GROUPS + BANK_GROUPS, GROUPS)
@@ -364,7 +364,7 @@ def tile_liquidmemorycell_pb_kernel(
         add_bias(b)
         multiply_gate(c, U_COLS)
         blend_change(a)
-        finish(a - 2)
+        finish(a - 4)
         decay_gate(b)
         update_gate(b)
         add_one_bias(c, D_COLS)
@@ -373,6 +373,7 @@ def tile_liquidmemorycell_pb_kernel(
         blend_kept(b)
         blend_sum(a)
         square_m(a)
+        finish(a - 3)
         add_one_bias(c, U_COLS)
         update_gate(c)
         blend_kept(c)
@@ -380,6 +381,7 @@ def tile_liquidmemorycell_pb_kernel(
         blend_change(c)
         norms(a)
         blend_gate(b)
+        finish(a - 2)
         blend_gate(c)
         blend_sum(b)
         blend_sum(c)

@@ -26,8 +26,9 @@ BANKS = GROUPS // BANK_GROUPS
 HALF_GROUPS = GROUPS // 2
 SORTED = 5
 UNSORTED = GROUPS - SORTED
-NORM_BATCHES = [(0, 2), (2, 4), (4, 6), (6, 8), (8, 10), (10, 12), (12, 14), (14, 16)]
-BATCH_MAX = 2
+NORM_BATCHES = [(0, 4), (4, 8), (8, 12), (12, 14), (14, 16)]
+BATCH_MAX = 4
+FINISHED_IN_STEP = {9: (0, 1), 10: (2, 3), 13: (4, 5), 14: (6, 7)}
 INPUT_BUFS = 8
 
 FLOPS = 2 * ROWS * DIN * GATES
@@ -86,9 +87,9 @@ def tile_liquidmemorycell_pb_kernel(
                 nc.sync.dma_start(out=inputs[t][:, 0:MEM], in_=h[rows, :])
                 for a, b in zip(cuts[:-1], cuts[1:]):
                     nc.sync.dma_start(out=inputs[t][:, a:b], in_=x[rows, a - MEM : b - MEM])
-            if live(t - 2):
-                rows = slice((t - 2) * P, (t - 1) * P)
-                nc.sync.dma_start(out=inputs[t - 2][:, DIN : DIN + MEM], in_=h_candidate[rows, :])
+            if live(t - 3):
+                rows = slice((t - 3) * P, (t - 2) * P)
+                nc.sync.dma_start(out=inputs[t - 3][:, DIN : DIN + MEM], in_=h_candidate[rows, :])
 
         w_words = keep.tile([P, GROUPS, GATES], U32, name="w_words", align_bytes=64)
 
@@ -155,7 +156,7 @@ def tile_liquidmemorycell_pb_kernel(
                 for i in range(BANK_GROUPS):
                     g = BANK_GROUPS * j + i
                     for u in range(2):
-                        if t == 0 or g < UNSORTED:
+                        if t < 2 or g < UNSORTED:
                             columns = words[:, g * WORDS + u : (g + 1) * WORDS : 2]
                         else:
                             columns = in_order[t][:, g - UNSORTED, u, :]
@@ -266,11 +267,16 @@ def tile_liquidmemorycell_pb_kernel(
             nc.vector.tensor_tensor(out=floored[:], in0=stats[b][:], in1=floors[:, :, 0 : end - first], op=ALU.max)
             powered[b] = keep.tile([P, 2, end - first], F32, name="powered%d" % b)
             nc.gpsimd.tensor_tensor(out=powered[b][:], in0=floored[:], in1=powers[:, :, 0 : end - first], op=ALU.pow)
-            if end < TILES:
-                scale[b] = keep.tile([P, end - first], F32, name="scale%d" % b)
-                nc.gpsimd.tensor_tensor(
-                    out=scale[b][:], in0=powered[b][:, 0, :], in1=powered[b][:, 1, :], op=ALU.mult
-                )
+
+        def factors(t):
+            b = batch_of[t]
+            first, end = NORM_BATCHES[b]
+            if t + 1 < end:
+                return
+            scale[b] = keep.tile([P, end - first], F32, name="scale%d" % b)
+            nc.vector.tensor_tensor(
+                out=scale[b][:], in0=powered[b][:, 0, :], in1=powered[b][:, 1, :], op=ALU.mult
+            )
 
         def end_of(t):
             return NORM_BATCHES[batch_of[t]][1]
@@ -315,14 +321,16 @@ def tile_liquidmemorycell_pb_kernel(
             if live(now):
                 copy_out(now, 2)
                 copy_out(now, 3)
-            if live(now - 7):
-                finish(now - 7)
+            for t in FINISHED_IN_STEP.get(now, ()):
+                finish(t)
             if live(now + 1) and now >= 2:
                 sort(now + 1)
             if live(now - 2):
                 blend_kept(now - 2)
             if live(now):
                 quantise(now, 0, HALF_GROUPS)
+            if live(now - 5):
+                factors(now - 5)
             if now == 1:
                 quantise(1, HALF_GROUPS, GROUPS)
             if live(now - 2):
@@ -331,8 +339,8 @@ def tile_liquidmemorycell_pb_kernel(
                 load_inputs(now - 2 + INPUT_BUFS)
             if now == 1:
                 spread_biases()
-            if now in (0, 1):
-                sort(now + 1)
+            if now == 1:
+                sort(2)
             if live(now - 1) and now != 2:
                 multiply(now - 1)
 
@@ -355,7 +363,6 @@ def tile_liquidmemorycell_pb_kernel(
         decay_gate(a)
         update_gate(a)
         square_m(a - 1)
-        finish(a - 5)
         quantise(c, 0, HALF_GROUPS)
         quantise(c, HALF_GROUPS, HALF_GROUPS + BANK_GROUPS)
         quantise(c, HALF_GROUPS + BANK_GROUPS, GROUPS)
@@ -364,7 +371,6 @@ def tile_liquidmemorycell_pb_kernel(
         add_bias(b)
         multiply_gate(c, U_COLS)
         blend_change(a)
-        finish(a - 4)
         decay_gate(b)
         update_gate(b)
         add_one_bias(c, D_COLS)
@@ -372,10 +378,13 @@ def tile_liquidmemorycell_pb_kernel(
         blend_gate(a)
         blend_kept(b)
         blend_sum(a)
+        factors(a - 2)
         square_m(a)
-        finish(a - 3)
         add_one_bias(c, U_COLS)
         update_gate(c)
+        finish(a - 5)
+        finish(a - 4)
+        finish(a - 3)
         blend_kept(c)
         blend_change(b)
         blend_change(c)
@@ -388,6 +397,7 @@ def tile_liquidmemorycell_pb_kernel(
         square_m(b)
         square_m(c)
         norms(c)
+        factors(a)
         finish(a - 1)
         finish(a)
         finish(b)

@@ -28,7 +28,6 @@ SORTED = 5
 UNSORTED = GROUPS - SORTED
 NORM_BATCHES = [(0, 4), (4, 8), (8, 12), (12, 14), (14, 16)]
 BATCH_MAX = 4
-FINISHED_IN_STEP = {9: (0, 1), 10: (2, 3), 13: (4, 5), 14: (6, 7)}
 INPUT_BUFS = 8
 
 FLOPS = 2 * ROWS * DIN * GATES
@@ -52,12 +51,12 @@ def tile_liquidmemorycell_pb_kernel(
         keep = stack.enter_context(tc.tile_pool(name="keep", bufs=1))
         arrivals = stack.enter_context(tc.tile_pool(name="arrivals", bufs=INPUT_BUFS))
         stage = stack.enter_context(tc.tile_pool(name="stage", bufs=3))
-        blends = stack.enter_context(tc.tile_pool(name="blends", bufs=9))
+        blends = stack.enter_context(tc.tile_pool(name="blends", bufs=11))
         leaving = stack.enter_context(tc.tile_pool(name="leaving", bufs=8))
         turned = stack.enter_context(tc.psum_pool(name="turned", bufs=6))
         sums = stack.enter_context(tc.psum_pool(name="sums", bufs=2))
 
-        w_scales = keep.tile([P, GROUPS, GATES], U8, name="w_scales", align_bytes=64)
+        w_scales = keep.tile([P, GROUPS, GATES], U8, name="w_scales", align_bytes=256)
         nc.vector.memset(w_scales[:].bitcast(I32), 0)
         bias_row = keep.tile([P, GATES], BF16, name="bias_row")
         nc.vector.memset(bias_row[:], 0.0)
@@ -91,7 +90,7 @@ def tile_liquidmemorycell_pb_kernel(
                 rows = slice((t - 3) * P, (t - 2) * P)
                 nc.sync.dma_start(out=inputs[t - 3][:, DIN : DIN + MEM], in_=h_candidate[rows, :])
 
-        w_words = keep.tile([P, GROUPS, GATES], U32, name="w_words", align_bytes=64)
+        w_words = keep.tile([P, GROUPS, GATES], U32, name="w_words", align_bytes=256)
 
         def load_scales(gate, scales):
             cols = slice(gate * MEM, (gate + 1) * MEM)
@@ -156,7 +155,7 @@ def tile_liquidmemorycell_pb_kernel(
                 for i in range(BANK_GROUPS):
                     g = BANK_GROUPS * j + i
                     for u in range(2):
-                        if t < 2 or g < UNSORTED:
+                        if t == 0 or g < UNSORTED:
                             columns = words[:, g * WORDS + u : (g + 1) * WORDS : 2]
                         else:
                             columns = in_order[t][:, g - UNSORTED, u, :]
@@ -164,7 +163,7 @@ def tile_liquidmemorycell_pb_kernel(
 
         def copy_out(t, j, copy=nc.scalar.copy):
             if j == 0:
-                grouped[t] = stage.tile([P, DIN], BF16, name="grouped%d" % t, tag="grouped", align_bytes=64)
+                grouped[t] = stage.tile([P, DIN], BF16, name="grouped%d" % t, tag="grouped", align_bytes=256)
             pairs = grouped[t][:].bitcast(F32).rearrange("p (g r u) -> p g r u", g=GROUPS, u=2)
             copy(
                 out=pairs[:, BANK_GROUPS * j : BANK_GROUPS * (j + 1), :, :],
@@ -179,8 +178,8 @@ def tile_liquidmemorycell_pb_kernel(
 
         def quantise(t, first, end):
             if first == 0:
-                codes[t] = stage.tile([P, GROUPS * P], U32, name="codes%d" % t, tag="codes", align_bytes=64)
-                c_scales[t] = stage.tile([P, GROUPS * P], U8, name="c_scales%d" % t, tag="c_scales", align_bytes=64)
+                codes[t] = stage.tile([P, GROUPS * P], U32, name="codes%d" % t, tag="codes", align_bytes=256)
+                c_scales[t] = stage.tile([P, GROUPS * P], U8, name="c_scales%d" % t, tag="c_scales", align_bytes=256)
             cols = slice(first * P, end * P)
             nc.vector.quantize_mx(
                 out=codes[t][:, cols].bitcast(FP8X4),
@@ -306,12 +305,12 @@ def tile_liquidmemorycell_pb_kernel(
                 quantise(now - 1, HALF_GROUPS, GROUPS)
             if live(now - 3):
                 blend_gate(now - 3)
+            if live(now - 4):
+                norms(now - 4)
             if live(now - 2):
                 add_bias(now - 2)
             if live(now - 3):
                 blend_sum(now - 3)
-            if live(now - 4):
-                norms(now - 4)
             if live(now):
                 copy_out(now, 0)
                 copy_out(now, 1)
@@ -321,8 +320,8 @@ def tile_liquidmemorycell_pb_kernel(
             if live(now):
                 copy_out(now, 2)
                 copy_out(now, 3)
-            for t in FINISHED_IN_STEP.get(now, ()):
-                finish(t)
+            if live(now - 9):
+                finish(now - 9)
             if live(now + 1) and now >= 2:
                 sort(now + 1)
             if live(now - 2):
@@ -339,8 +338,8 @@ def tile_liquidmemorycell_pb_kernel(
                 load_inputs(now - 2 + INPUT_BUFS)
             if now == 1:
                 spread_biases()
-            if now == 1:
-                sort(2)
+            if now in (0, 1):
+                sort(now + 1)
             if live(now - 1) and now != 2:
                 multiply(now - 1)
 
@@ -355,19 +354,22 @@ def tile_liquidmemorycell_pb_kernel(
         quantise(b, HALF_GROUPS, GROUPS)
         multiply(b)
         blend_gate(a - 1)
+        norms(a - 2)
         add_bias(a)
         blend_sum(a - 1)
-        norms(a - 2)
         for j in range(BANKS):
             copy_out(c, j)
         decay_gate(a)
         update_gate(a)
         square_m(a - 1)
+        finish(a - 7)
+        finish(a - 6)
         quantise(c, 0, HALF_GROUPS)
         quantise(c, HALF_GROUPS, HALF_GROUPS + BANK_GROUPS)
         quantise(c, HALF_GROUPS + BANK_GROUPS, GROUPS)
         multiply_gate(c, D_COLS)
         blend_kept(a)
+        factors(a - 2)
         add_bias(b)
         multiply_gate(c, U_COLS)
         blend_change(a)
@@ -375,14 +377,13 @@ def tile_liquidmemorycell_pb_kernel(
         update_gate(b)
         add_one_bias(c, D_COLS)
         decay_gate(c)
+        finish(a - 5)
         blend_gate(a)
         blend_kept(b)
         blend_sum(a)
-        factors(a - 2)
         square_m(a)
         add_one_bias(c, U_COLS)
         update_gate(c)
-        finish(a - 5)
         finish(a - 4)
         finish(a - 3)
         blend_kept(c)

@@ -28,6 +28,8 @@ SORTED = 5
 UNSORTED = GROUPS - SORTED
 NORM_BATCHES = [(0, 4), (4, 8), (8, 12), (12, 14), (14, 16)]
 BATCH_MAX = 4
+LATE = 4
+FIRST_LATE = TILES - LATE
 INPUT_BUFS = 8
 
 FLOPS = 2 * ROWS * DIN * GATES
@@ -138,6 +140,8 @@ def tile_liquidmemorycell_pb_kernel(
             stats.append(keep.tile([P, 2, end - first], F32, name="stats%d" % b))
             for t in range(first, end):
                 batch_of[t], place_of[t] = b, t - first
+        late_h = keep.tile([P, LATE], F32, name="late_h")
+        late_h_norm = keep.tile([P, LATE], F32, name="late_h_norm")
         powered = {}
 
         def sort(t):
@@ -172,9 +176,9 @@ def tile_liquidmemorycell_pb_kernel(
 
         def square_h(t):
             h_squares = stage.tile([P, MEM], BF16, name="h_squares%d" % t, tag="h_squares")
-            nc.scalar.activation(
-                out=h_squares[:], in_=inputs[t][:, 0:MEM], func=ACT.Square, accum_out=stats[batch_of[t]][:, 0, place_of[t] : place_of[t] + 1]
-            )
+            b, i = batch_of[t], place_of[t]
+            h_stat = late_h[:, t - FIRST_LATE : t - FIRST_LATE + 1] if t >= FIRST_LATE else stats[b][:, 0, i : i + 1]
+            nc.scalar.activation(out=h_squares[:], in_=inputs[t][:, 0:MEM], func=ACT.Square, accum_out=h_stat)
 
         def quantise(t, first, end):
             if first == 0:
@@ -262,10 +266,26 @@ def tile_liquidmemorycell_pb_kernel(
             first, end = NORM_BATCHES[b]
             if t + 1 < end:
                 return
+            parts = slice(1, 2) if t >= FIRST_LATE else slice(0, 2)
             floored = keep.tile([P, 2, end - first], F32, name="floored%d" % b)
-            nc.vector.tensor_tensor(out=floored[:], in0=stats[b][:], in1=floors[:, :, 0 : end - first], op=ALU.max)
+            nc.vector.tensor_tensor(
+                out=floored[:, parts, :], in0=stats[b][:, parts, :], in1=floors[:, parts, 0 : end - first], op=ALU.max
+            )
             powered[b] = keep.tile([P, 2, end - first], F32, name="powered%d" % b)
-            nc.gpsimd.tensor_tensor(out=powered[b][:], in0=floored[:], in1=powers[:, :, 0 : end - first], op=ALU.pow)
+            nc.gpsimd.tensor_tensor(
+                out=powered[b][:, parts, :], in0=floored[:, parts, :], in1=powers[:, parts, 0 : end - first], op=ALU.pow
+            )
+
+        def late_h_norms():
+            floored = keep.tile([P, LATE], F32, name="late_h_floored")
+            nc.vector.tensor_tensor(out=floored[:], in0=late_h[:], in1=floors[:, 0, :], op=ALU.max)
+            nc.gpsimd.tensor_tensor(out=late_h_norm[:], in0=floored[:], in1=powers[:, 0, :], op=ALU.pow)
+
+        def h_norm(t, count):
+            b, i = batch_of[t], place_of[t]
+            if t >= FIRST_LATE:
+                return late_h_norm[:, t - FIRST_LATE : t - FIRST_LATE + count]
+            return powered[b][:, 0, i : i + count]
 
         def factors(t):
             b = batch_of[t]
@@ -274,7 +294,7 @@ def tile_liquidmemorycell_pb_kernel(
                 return
             scale[b] = keep.tile([P, end - first], F32, name="scale%d" % b)
             nc.vector.tensor_tensor(
-                out=scale[b][:], in0=powered[b][:, 0, :], in1=powered[b][:, 1, :], op=ALU.mult
+                out=scale[b][:], in0=h_norm(first, end - first), in1=powered[b][:, 1, :], op=ALU.mult
             )
 
         def end_of(t):
@@ -287,7 +307,7 @@ def tile_liquidmemorycell_pb_kernel(
                 nc.scalar.activation(out=result[:], in_=blend[t][:], func=ACT.Copy, scale=scale[b][:, i : i + 1])
             else:
                 nc.vector.tensor_scalar(
-                    out=result[:], in0=blend[t][:], scalar1=powered[b][:, 0, i : i + 1],
+                    out=result[:], in0=blend[t][:], scalar1=h_norm(t, 1),
                     scalar2=powered[b][:, 1, i : i + 1], op0=ALU.mult, op1=ALU.mult,
                 )
             nc.sync.dma_start(out=out[t * P : (t + 1) * P, :], in_=result[:])
@@ -370,6 +390,7 @@ def tile_liquidmemorycell_pb_kernel(
         multiply_gate(c, D_COLS)
         blend_kept(a)
         factors(a - 2)
+        late_h_norms()
         add_bias(b)
         multiply_gate(c, U_COLS)
         blend_change(a)

@@ -142,7 +142,7 @@ def tile_liquidmemorycell_pb_kernel(
                 batch_of[t], place_of[t] = b, t - first
         late_h = keep.tile([P, LATE], F32, name="late_h")
         late_h_norm = keep.tile([P, LATE], F32, name="late_h_norm")
-        powered = {}
+        powered, floored, inverted = {}, {}, {}
 
         def sort(t):
             in_order[t] = stage.tile([P, SORTED, 2, P], F32, name="in_order%d" % t, tag="in_order")
@@ -267,25 +267,41 @@ def tile_liquidmemorycell_pb_kernel(
             if t + 1 < end:
                 return
             parts = slice(1, 2) if t >= FIRST_LATE else slice(0, 2)
-            floored = keep.tile([P, 2, end - first], F32, name="floored%d" % b)
+            floored[b] = keep.tile([P, 2, end - first], F32, name="floored%d" % b)
             nc.vector.tensor_tensor(
-                out=floored[:, parts, :], in0=stats[b][:, parts, :], in1=floors[:, parts, 0 : end - first], op=ALU.max
+                out=floored[b][:, parts, :], in0=stats[b][:, parts, :], in1=floors[:, parts, 0 : end - first], op=ALU.max
             )
-            powered[b] = keep.tile([P, 2, end - first], F32, name="powered%d" % b)
-            nc.gpsimd.tensor_tensor(
-                out=powered[b][:, parts, :], in0=floored[:, parts, :], in1=powers[:, parts, 0 : end - first], op=ALU.pow
-            )
+            if t >= FIRST_LATE:
+                powered[b] = keep.tile([P, end - first], F32, name="powered%d" % b)
+                nc.gpsimd.tensor_tensor(
+                    out=powered[b][:], in0=floored[b][:, 1, :], in1=powers[:, 1, 0 : end - first], op=ALU.pow
+                )
+
+        def inverse(t):
+            b = batch_of[t]
+            first, end = NORM_BATCHES[b]
+            if t + 1 == end:
+                inverted[b] = keep.tile([P, end - first], F32, name="inverted%d" % b)
+                nc.vector.reciprocal(out=inverted[b][:], in_=floored[b][:, 1, :])
+
+        def ratios(t):
+            b = batch_of[t]
+            first, end = NORM_BATCHES[b]
+            if t + 1 == end:
+                squares = keep.tile([P, end - first], F32, name="ratio%d" % b)
+                nc.vector.tensor_tensor(out=squares[:], in0=floored[b][:, 0, :], in1=inverted[b][:], op=ALU.mult)
+                scale[b] = keep.tile([P, end - first], F32, name="scale%d" % b)
+                nc.gpsimd.tensor_tensor(
+                    out=scale[b][:], in0=squares[:], in1=powers[:, 0, 0 : end - first], op=ALU.pow
+                )
 
         def late_h_norms():
-            floored = keep.tile([P, LATE], F32, name="late_h_floored")
-            nc.vector.tensor_tensor(out=floored[:], in0=late_h[:], in1=floors[:, 0, :], op=ALU.max)
-            nc.gpsimd.tensor_tensor(out=late_h_norm[:], in0=floored[:], in1=powers[:, 0, :], op=ALU.pow)
+            late_h_floored = keep.tile([P, LATE], F32, name="late_h_floored")
+            nc.vector.tensor_tensor(out=late_h_floored[:], in0=late_h[:], in1=floors[:, 0, :], op=ALU.max)
+            nc.gpsimd.tensor_tensor(out=late_h_norm[:], in0=late_h_floored[:], in1=powers[:, 0, :], op=ALU.pow)
 
         def h_norm(t, count):
-            b, i = batch_of[t], place_of[t]
-            if t >= FIRST_LATE:
-                return late_h_norm[:, t - FIRST_LATE : t - FIRST_LATE + count]
-            return powered[b][:, 0, i : i + count]
+            return late_h_norm[:, t - FIRST_LATE : t - FIRST_LATE + count]
 
         def factors(t):
             b = batch_of[t]
@@ -294,7 +310,7 @@ def tile_liquidmemorycell_pb_kernel(
                 return
             scale[b] = keep.tile([P, end - first], F32, name="scale%d" % b)
             nc.vector.tensor_tensor(
-                out=scale[b][:], in0=h_norm(first, end - first), in1=powered[b][:, 1, :], op=ALU.mult
+                out=scale[b][:], in0=h_norm(first, end - first), in1=powered[b][:], op=ALU.mult
             )
 
         def end_of(t):
@@ -308,7 +324,7 @@ def tile_liquidmemorycell_pb_kernel(
             else:
                 nc.vector.tensor_scalar(
                     out=result[:], in0=blend[t][:], scalar1=h_norm(t, 1),
-                    scalar2=powered[b][:, 1, i : i + 1], op0=ALU.mult, op1=ALU.mult,
+                    scalar2=powered[b][:, i : i + 1], op0=ALU.mult, op1=ALU.mult,
                 )
             nc.sync.dma_start(out=out[t * P : (t + 1) * P, :], in_=result[:])
 
@@ -327,6 +343,8 @@ def tile_liquidmemorycell_pb_kernel(
                 blend_gate(now - 3)
             if live(now - 4):
                 norms(now - 4)
+            if live(now - 5):
+                ratios(now - 5)
             if live(now - 2):
                 add_bias(now - 2)
             if live(now - 3):
@@ -348,8 +366,8 @@ def tile_liquidmemorycell_pb_kernel(
                 blend_kept(now - 2)
             if live(now):
                 quantise(now, 0, HALF_GROUPS)
-            if live(now - 5):
-                factors(now - 5)
+            if live(now - 4):
+                inverse(now - 4)
             if now == 1:
                 quantise(1, HALF_GROUPS, GROUPS)
             if live(now - 2):
@@ -376,7 +394,9 @@ def tile_liquidmemorycell_pb_kernel(
         blend_gate(a - 1)
         norms(a - 2)
         add_bias(a)
+        inverse(a - 2)
         blend_sum(a - 1)
+        ratios(a - 2)
         for j in range(BANKS):
             copy_out(c, j)
         decay_gate(a)
@@ -389,7 +409,6 @@ def tile_liquidmemorycell_pb_kernel(
         quantise(c, HALF_GROUPS + BANK_GROUPS, GROUPS)
         multiply_gate(c, D_COLS)
         blend_kept(a)
-        factors(a - 2)
         late_h_norms()
         add_bias(b)
         multiply_gate(c, U_COLS)

import math
from contextlib import ExitStack

import concourse.mybir as mybir
from concourse.masks import make_identity

F32 = mybir.dt.float32
BF16 = mybir.dt.bfloat16
I32 = mybir.dt.int32
U32 = mybir.dt.uint32
U8 = mybir.dt.uint8
FP8X4 = mybir.dt.float8_e4m3fn_x4
ALU = mybir.AluOpType
ACT = mybir.ActivationFunctionType

P = 128
ROWS, IN_DIM, MEM = 2048, 3840, 256
DIN = MEM + IN_DIM
GATES = 2 * MEM
TILES = ROWS // P
K_PASS = 4 * P
GROUPS = DIN // K_PASS
WORDS = K_PASS // 2
BANK_GROUPS = 2
BANKS = GROUPS // BANK_GROUPS
HALF_GROUPS = GROUPS // 2
SORTED = 5
UNSORTED = GROUPS - SORTED
NORM_BATCHES = [(0, 4), (4, 8), (8, 12), (12, 14), (14, 16)]
BATCH_MAX = 4
LATE = 4
FIRST_LATE = TILES - LATE
INPUT_BUFS = 8

FLOPS = 2 * ROWS * DIN * GATES

TS_FLOOR = 0.1 + 1e-6
TS_SPAN = 10.0 - 0.1
SHIFT = math.log((TS_FLOOR + TS_SPAN) / TS_FLOOR)
S_OFFSET = TS_FLOOR / TS_SPAN
M_GAIN = TS_FLOOR * (TS_FLOOR + TS_SPAN) / TS_SPAN
H_NORM_FLOOR = 1e-6
M_NORM_FLOOR = 1e-12 * M_GAIN


def tile_liquidmemorycell_pb_kernel(
    tc, x, h, h_candidate, Wd_words, Wd_scales, bd, Wu_words, Wu_scales, bu, out
):
    nc = tc.nc

    with ExitStack() as stack:
        stack.enter_context(tc.manual_schedule())
        keep = stack.enter_context(tc.tile_pool(name="keep", bufs=1))
        arrivals = stack.enter_context(tc.tile_pool(name="arrivals", bufs=INPUT_BUFS))
        stage = stack.enter_context(tc.tile_pool(name="stage", bufs=3))
        blends = stack.enter_context(tc.tile_pool(name="blends", bufs=11))
        leaving = stack.enter_context(tc.tile_pool(name="leaving", bufs=8))
        turned = stack.enter_context(tc.psum_pool(name="turned", bufs=6))
        sums = stack.enter_context(tc.psum_pool(name="sums", bufs=2))

        w_scales = keep.tile([P, GROUPS, GATES], U8, name="w_scales", align_bytes=256)
        nc.vector.memset(w_scales[:].bitcast(I32), 0)
        bias_row = keep.tile([P, GATES], BF16, name="bias_row")
        nc.vector.memset(bias_row[:], 0.0)
        ones = keep.tile([P, P], BF16, name="ones")
        nc.vector.memset(ones[:], 1.0)
        floors = keep.tile([P, 2, BATCH_MAX], F32, name="floors")
        nc.vector.memset(floors[:, 0, :], H_NORM_FLOOR * H_NORM_FLOOR)
        nc.vector.memset(floors[:, 1, :], M_NORM_FLOOR * M_NORM_FLOOR)
        powers = keep.tile([P, 2, BATCH_MAX], F32, name="powers")
        nc.vector.memset(powers[:, 0, :], 0.5)
        nc.vector.memset(powers[:, 1, :], -0.5)
        identity = keep.tile([P, P], F32, name="identity")
        make_identity(nc, identity[:])

        table_warmer = keep.tile([P, 1], F32, name="table_warmer")
        nc.scalar.activation(out=table_warmer[:], in_=powers[:, 0, 0:1], func=ACT.Sigmoid)

        inputs = {}

        def live(t):
            return 0 <= t < TILES

        def load_inputs(t, cuts=(MEM, DIN)):
            if live(t):
                rows = slice(t * P, (t + 1) * P)
                inputs[t] = arrivals.tile([P, DIN + MEM], BF16, name="inputs%d" % t, tag="inputs")
                nc.sync.dma_start(out=inputs[t][:, 0:MEM], in_=h[rows, :])
                for a, b in zip(cuts[:-1], cuts[1:]):
                    nc.sync.dma_start(out=inputs[t][:, a:b], in_=x[rows, a - MEM : b - MEM])
            if live(t - 3):
                rows = slice((t - 3) * P, (t - 2) * P)
                nc.sync.dma_start(out=inputs[t - 3][:, DIN : DIN + MEM], in_=h_candidate[rows, :])

        w_words = keep.tile([P, GROUPS, GATES], U32, name="w_words", align_bytes=256)

        def load_scales(gate, scales):
            cols = slice(gate * MEM, (gate + 1) * MEM)
            for quadrant in range(4):
                nc.sync.dma_start(
                    out=w_scales[32 * quadrant : 32 * quadrant + 4, :, cols].bitcast(I32),
                    in_=scales[:, 4 * quadrant : 4 * quadrant + 4, :].rearrange("g r n -> r g n").bitcast(I32),
                )

        def load_words(gate, words, groups):
            cols = slice(gate * MEM, (gate + 1) * MEM)
            nc.sync.dma_start(
                out=w_words[:, groups, cols].bitcast(I32),
                in_=words[groups].rearrange("g p n i -> p g (n i)").bitcast(I32),
            )

        load_inputs(0, (MEM, DIN // 2, DIN))
        load_scales(0, Wd_scales)
        load_inputs(1)
        nc.scalar.dma_start(out=bias_row[0:1, 0:MEM], in_=bd.unsqueeze(0))
        nc.scalar.dma_start(out=bias_row[0:1, MEM:GATES], in_=bu.unsqueeze(0))
        first_half, last_half = slice(0, HALF_GROUPS), slice(HALF_GROUPS, GROUPS)
        load_words(0, Wd_words, first_half)
        load_words(1, Wu_words, first_half)
        load_scales(1, Wu_scales)
        load_words(0, Wd_words, last_half)
        load_words(1, Wu_words, last_half)
        for t in range(2, INPUT_BUFS):
            load_inputs(t)

        bias = keep.tile([P, GATES], F32, name="bias")

        def spread_biases():
            bias_sums = sums.tile([P, GATES], F32, name="bias_sums", tag="sums")
            nc.tensor.matmul(out=bias_sums[:], lhsT=ones[:], rhs=bias_row[:], start=True, stop=True)
            nc.vector.tensor_scalar(
                out=bias[:, 0:MEM], in0=bias_sums[:, 0:MEM], scalar1=SHIFT, scalar2=None, op0=ALU.add
            )
            nc.vector.tensor_copy(out=bias[:, MEM:GATES], in_=bias_sums[:, MEM:GATES])

        in_order, banks, grouped, codes, c_scales, gate_sums = {}, {}, {}, {}, {}, {}
        logits, shifted, update, kept, change, blend, scale = {}, {}, {}, {}, {}, {}, {}
        stats, batch_of, place_of = [], {}, {}
        for b, (first, end) in enumerate(NORM_BATCHES):
            stats.append(keep.tile([P, 2, end - first], F32, name="stats%d" % b))
            for t in range(first, end):
                batch_of[t], place_of[t] = b, t - first
        late_h = keep.tile([P, LATE], F32, name="late_h")
        late_h_norm = keep.tile([P, LATE], F32, name="late_h_norm")
        powered, floored, inverted = {}, {}, {}

        def sort(t):
            in_order[t] = stage.tile([P, SORTED, 2, P], F32, name="in_order%d" % t, tag="in_order")
            as_loaded = inputs[t][:, UNSORTED * K_PASS : DIN].bitcast(F32)
            nc.vector.tensor_copy(
                out=in_order[t][:].rearrange("p g u w -> p u g w"),
                in_=as_loaded.rearrange("p (g w u) -> p u g w", g=SORTED, u=2),
            )

        def transpose(t):
            words = inputs[t][:, 0:DIN].bitcast(F32)
            for j in range(BANKS):
                banks[t, j] = turned.tile([P, BANK_GROUPS, 2, P], F32, name="turned%d_%d" % (t, j), tag="turned")
                for i in range(BANK_GROUPS):
                    g = BANK_GROUPS * j + i
                    for u in range(2):
                        if t == 0 or g < UNSORTED:
                            columns = words[:, g * WORDS + u : (g + 1) * WORDS : 2]
                        else:
                            columns = in_order[t][:, g - UNSORTED, u, :]
                        nc.tensor.transpose(banks[t, j][:, i, u, :], columns, identity[:])

        def copy_out(t, j, copy=nc.scalar.copy):
            if j == 0:
                grouped[t] = stage.tile([P, DIN], BF16, name="grouped%d" % t, tag="grouped", align_bytes=256)
            pairs = grouped[t][:].bitcast(F32).rearrange("p (g r u) -> p g r u", g=GROUPS, u=2)
            copy(
                out=pairs[:, BANK_GROUPS * j : BANK_GROUPS * (j + 1), :, :],
                in_=banks[t, j][:].rearrange("p g u r -> p g r u"),
            )

        def square_h(t):
            h_squares = stage.tile([P, MEM], BF16, name="h_squares%d" % t, tag="h_squares")
            b, i = batch_of[t], place_of[t]
            h_stat = late_h[:, t - FIRST_LATE : t - FIRST_LATE + 1] if t >= FIRST_LATE else stats[b][:, 0, i : i + 1]
            nc.scalar.activation(out=h_squares[:], in_=inputs[t][:, 0:MEM], func=ACT.Square, accum_out=h_stat)

        def quantise(t, first, end):
            if first == 0:
                codes[t] = stage.tile([P, GROUPS * P], U32, name="codes%d" % t, tag="codes", align_bytes=256)
                c_scales[t] = stage.tile([P, GROUPS * P], U8, name="c_scales%d" % t, tag="c_scales", align_bytes=256)
            cols = slice(first * P, end * P)
            nc.vector.quantize_mx(
                out=codes[t][:, cols].bitcast(FP8X4),
                scales=c_scales[t][:, cols],
                in_=grouped[t][:, first * K_PASS : end * K_PASS],
            )

        def multiply(t):
            gate_sums[t] = sums.tile([P, GATES], F32, name="gate_sums%d" % t, tag="sums")
            multiply_into(t, gate_sums[t][:], slice(0, GATES))

        def multiply_into(t, out, columns):
            for g in range(GROUPS):
                rows = slice(g * P, (g + 1) * P)
                nc.tensor.matmul_mx(
                    out=out,
                    lhsT=codes[t][:, rows].bitcast(FP8X4),
                    lhsT_scale=c_scales[t][:, rows],
                    rhs=w_words[:, g, columns].bitcast(FP8X4),
                    rhs_scale=w_scales[:, g, columns],
                    start=(g == 0),
                    stop=(g == GROUPS - 1),
                )

        def add_bias(t):
            logits[t] = stage.tile([P, GATES], F32, name="logits%d" % t, tag="logits")
            nc.vector.tensor_tensor(out=logits[t][:], in0=gate_sums[t][:], in1=bias[:], op=ALU.add)

        D_COLS, U_COLS = slice(0, MEM), slice(MEM, GATES)

        def decay_gate(t):
            shifted[t] = stage.tile([P, MEM], F32, name="shifted%d" % t, tag="shifted")
            nc.scalar.activation(out=shifted[t][:], in_=logits[t][:, D_COLS], func=ACT.Sigmoid, scale=-1.0)

        def update_gate(t):
            update[t] = stage.tile([P, MEM], F32, name="update%d" % t, tag="update")
            nc.scalar.activation(out=update[t][:], in_=logits[t][:, U_COLS], func=ACT.Sigmoid)

        def multiply_gate(t, columns):
            gate_sums[t, columns.start] = sums.tile(
                [P, MEM], F32, name="gate_sums%d_%d" % (t, columns.start), tag="sums"
            )
            multiply_into(t, gate_sums[t, columns.start][:], columns)

        def add_one_bias(t, columns):
            if columns.start == 0:
                logits[t] = stage.tile([P, GATES], F32, name="logits%d" % t, tag="logits")
            nc.vector.tensor_tensor(
                out=logits[t][:, columns], in0=gate_sums[t, columns.start][:], in1=bias[:, columns], op=ALU.add
            )

        def blend_kept(t):
            kept[t] = stage.tile([P, MEM], F32, name="kept%d" % t, tag="kept")
            nc.vector.scalar_tensor_tensor(
                out=kept[t][:], in0=shifted[t][:], scalar=S_OFFSET, in1=inputs[t][:, 0:MEM],
                op0=ALU.add, op1=ALU.mult,
            )

        def blend_change(t):
            change[t] = stage.tile([P, MEM], F32, name="change%d" % t, tag="change")
            nc.vector.scalar_tensor_tensor(
                out=change[t][:], in0=inputs[t][:, DIN : DIN + MEM], scalar=M_GAIN, in1=kept[t][:],
                op0=ALU.mult, op1=ALU.subtract,
            )

        def blend_gate(t):
            nc.vector.tensor_tensor(out=change[t][:], in0=change[t][:], in1=update[t][:], op=ALU.mult)

        def blend_sum(t):
            blend[t] = blends.tile([P, MEM], F32, name="blend%d" % t, tag="blend")
            nc.vector.tensor_tensor(out=blend[t][:], in0=change[t][:], in1=kept[t][:], op=ALU.add)

        def square_m(t):
            m_squares = stage.tile([P, MEM], BF16, name="m_squares%d" % t, tag="m_squares")
            nc.scalar.activation(out=m_squares[:], in_=blend[t][:], func=ACT.Square,
                                 accum_out=stats[batch_of[t]][:, 1, place_of[t] : place_of[t] + 1])

        def norms(t):
            b = batch_of[t]
            first, end = NORM_BATCHES[b]
            if t + 1 < end:
                return
            parts = slice(1, 2) if t >= FIRST_LATE else slice(0, 2)
            floored[b] = keep.tile([P, 2, end - first], F32, name="floored%d" % b)
            nc.vector.tensor_tensor(
                out=floored[b][:, parts, :], in0=stats[b][:, parts, :], in1=floors[:, parts, 0 : end - first], op=ALU.max
            )
            if t >= FIRST_LATE:
                powered[b] = keep.tile([P, end - first], F32, name="powered%d" % b)
                nc.gpsimd.tensor_tensor(
                    out=powered[b][:], in0=floored[b][:, 1, :], in1=powers[:, 1, 0 : end - first], op=ALU.pow
                )

        def inverse(t):
            b = batch_of[t]
            first, end = NORM_BATCHES[b]
            if t + 1 == end:
                inverted[b] = keep.tile([P, end - first], F32, name="inverted%d" % b)
                nc.vector.reciprocal(out=inverted[b][:], in_=floored[b][:, 1, :])

        def ratios(t):
            b = batch_of[t]
            first, end = NORM_BATCHES[b]
            if t + 1 == end:
                squares = keep.tile([P, end - first], F32, name="ratio%d" % b)
                nc.vector.tensor_tensor(out=squares[:], in0=floored[b][:, 0, :], in1=inverted[b][:], op=ALU.mult)
                scale[b] = keep.tile([P, end - first], F32, name="scale%d" % b)
                nc.gpsimd.tensor_tensor(
                    out=scale[b][:], in0=squares[:], in1=powers[:, 0, 0 : end - first], op=ALU.pow
                )

        def late_h_norms():
            late_h_floored = keep.tile([P, LATE], F32, name="late_h_floored")
            nc.vector.tensor_tensor(out=late_h_floored[:], in0=late_h[:], in1=floors[:, 0, :], op=ALU.max)
            nc.gpsimd.tensor_tensor(out=late_h_norm[:], in0=late_h_floored[:], in1=powers[:, 0, :], op=ALU.pow)

        def h_norm(t, count):
            return late_h_norm[:, t - FIRST_LATE : t - FIRST_LATE + count]

        def factors(t):
            b = batch_of[t]
            first, end = NORM_BATCHES[b]
            if t + 1 < end:
                return
            scale[b] = keep.tile([P, end - first], F32, name="scale%d" % b)
            nc.vector.tensor_tensor(
                out=scale[b][:], in0=h_norm(first, end - first), in1=powered[b][:], op=ALU.mult
            )

        def end_of(t):
            return NORM_BATCHES[batch_of[t]][1]

        def finish(t):
            b, i = batch_of[t], place_of[t]
            result = leaving.tile([P, MEM], F32, name="result%d" % t, tag="result")
            if end_of(t) < TILES:
                nc.scalar.activation(out=result[:], in_=blend[t][:], func=ACT.Copy, scale=scale[b][:, i : i + 1])
            else:
                nc.vector.tensor_scalar(
                    out=result[:], in0=blend[t][:], scalar1=h_norm(t, 1),
                    scalar2=powered[b][:, i : i + 1], op0=ALU.mult, op1=ALU.mult,
                )
            nc.sync.dma_start(out=out[t * P : (t + 1) * P, :], in_=result[:])

        def step(now):
            if now == 2:
                multiply(1)
            if live(now):
                transpose(now)
            if live(now - 4):
                square_m(now - 4)
            if live(now):
                square_h(now)
            if live(now - 1) and now != 2:
                quantise(now - 1, HALF_GROUPS, GROUPS)
            if live(now - 3):
                blend_gate(now - 3)
            if live(now - 4):
                norms(now - 4)
            if live(now - 5):
                ratios(now - 5)
            if live(now - 2):
                add_bias(now - 2)
            if live(now - 3):
                blend_sum(now - 3)
            if live(now):
                copy_out(now, 0)
                copy_out(now, 1)
            if live(now - 2):
                decay_gate(now - 2)
                update_gate(now - 2)
            if live(now):
                copy_out(now, 2)
                copy_out(now, 3)
            if live(now - 9):
                finish(now - 9)
            if live(now + 1) and now >= 2:
                sort(now + 1)
            if live(now - 2):
                blend_kept(now - 2)
            if live(now):
                quantise(now, 0, HALF_GROUPS)
            if live(now - 4):
                inverse(now - 4)
            if now == 1:
                quantise(1, HALF_GROUPS, GROUPS)
            if live(now - 2):
                blend_change(now - 2)
            if live(now - 2):
                load_inputs(now - 2 + INPUT_BUFS)
            if now == 1:
                spread_biases()
            if now in (0, 1):
                sort(now + 1)
            if live(now - 1) and now != 2:
                multiply(now - 1)

        for now in range(-1, TILES - 1):
            step(now)

        a, b, c = TILES - 3, TILES - 2, TILES - 1

        transpose(c)
        square_m(a - 2)
        square_h(c)
        quantise(b, HALF_GROUPS, GROUPS)
        multiply(b)
        blend_gate(a - 1)
        norms(a - 2)
        add_bias(a)
        inverse(a - 2)
        blend_sum(a - 1)
        ratios(a - 2)
        for j in range(BANKS):
            copy_out(c, j)
        decay_gate(a)
        update_gate(a)
        square_m(a - 1)
        finish(a - 7)
        finish(a - 6)
        quantise(c, 0, HALF_GROUPS)
        quantise(c, HALF_GROUPS, HALF_GROUPS + BANK_GROUPS)
        quantise(c, HALF_GROUPS + BANK_GROUPS, GROUPS)
        multiply_gate(c, D_COLS)
        blend_kept(a)
        late_h_norms()
        add_bias(b)
        multiply_gate(c, U_COLS)
        blend_change(a)
        decay_gate(b)
        update_gate(b)
        add_one_bias(c, D_COLS)
        decay_gate(c)
        finish(a - 5)
        blend_gate(a)
        blend_kept(b)
        blend_sum(a)
        square_m(a)
        add_one_bias(c, U_COLS)
        update_gate(c)
        finish(a - 4)
        finish(a - 3)
        blend_kept(c)
        blend_change(b)
        blend_change(c)
        norms(a)
        blend_gate(b)
        finish(a - 2)
        blend_gate(c)
        blend_sum(b)
        blend_sum(c)
        square_m(b)
        square_m(c)
        norms(c)
        factors(a)
        finish(a - 1)
        finish(a)
        finish(b)
        finish(c)
